import numpy as np
import ml_dtypes


def mxq(x, axis, fmt="e4m3"):
    dtype, down = {"e4m3": (ml_dtypes.float8_e4m3fn, 7), "e5m2": (ml_dtypes.float8_e5m2, 14)}[fmt]
    v = np.moveaxis(np.asarray(x, np.float32).astype(ml_dtypes.bfloat16).astype(np.float64), axis, -1)
    blocks = v.reshape(v.shape[:-1] + (-1, 32))
    amax = np.abs(blocks).max(-1, keepdims=True)
    byte = np.maximum(np.where(amax > 0, np.frexp(amax)[1] - 1 + 127, 0) - down, 1)
    scale = np.exp2(byte - 127.0)
    codes = (blocks / scale).astype(np.float32).astype(dtype).astype(np.float64)
    return np.moveaxis((codes * scale).reshape(v.shape), -1, axis)


WIDE = False


def mx_kscale(k):
    if not WIDE:
        return np.ones(k)
    levels = np.array([10, -10, 5, -5, 0])
    a = np.random.permutation(np.resize(levels, k // 512 * 4)).reshape(k // 512, 4)
    idx = np.arange(k)
    return np.exp2(a[idx // 512, idx % 128 // 32])


BF16 = ml_dtypes.bfloat16


def bf(x):
    return np.asarray(x, np.float32).astype(BF16)


def f64(x):
    return np.asarray(x).astype(np.float64)


B, N, R = 1024, 1024, 4


def setup_inputs():
    t = mx_kscale(N)
    return {"x": bf(np.random.standard_normal((B, N)) / t),
            "q_prev": bf(np.random.standard_normal((N, N)) / np.sqrt(N) * t),
            "v": bf(np.random.standard_normal(N))}


def reference(x, q_prev, v):
    v = f64(v)
    u = v / np.sqrt(np.sum(v * v))
    h = np.eye(N) - 2.0 * (u[:, None] * u[None, :])
    w = mxq(h, 1, "e4m3") @ mxq(f64(q_prev), 0, "e4m3")
    return mxq(f64(x), 1, "e4m3") @ mxq(w, 1, "e4m3").T

@@ -1,0 +1,222 @@
+from contextlib import ExitStack
+
+import concourse.mybir as mybir
+from concourse.masks import make_identity
+
+FLOPS = 2 * 2 * 1024 * 1024 * 1024
+
+F32 = mybir.dt.float32
+BF16 = mybir.dt.bfloat16
+U32 = mybir.dt.uint32
+U8 = mybir.dt.uint8
+FP8X4 = mybir.dt.float8_e4m3fn_x4
+MULT = mybir.AluOpType.mult
+ADD = mybir.AluOpType.add
+COPY = mybir.ActivationFunctionType.Copy
+
+P = 128
+N = 1024
+
+
+def tile_householderlinear_pa_kernel(tc, x, q_prev, v, out):
+    nc = tc.nc
+    with ExitStack() as ctx:
+        const = ctx.enter_context(tc.tile_pool(name="const", bufs=1))
+        keep = ctx.enter_context(tc.tile_pool(name="keep", bufs=1))
+        stage = ctx.enter_context(tc.tile_pool(name="stage", bufs=3))
+        psum_a = ctx.enter_context(tc.psum_pool(name="psum_a", bufs=4))
+        psum_b = ctx.enter_context(tc.psum_pool(name="psum_b", bufs=3))
+        psum_s = ctx.enter_context(tc.psum_pool(name="psum_s", bufs=1))
+
+        vcol = const.tile([P, 8], BF16)
+        nc.scalar.dma_start(out=vcol[:], in_=v.rearrange("(p m) -> p m", m=8))
+        vrow = const.tile([P, N], BF16)
+        nc.vector.memset(vrow[:], 0.0)
+        nc.scalar.dma_start(out=vrow[0:1, :], in_=v.rearrange("(o n) -> o n", o=1))
+
+        raw_q = keep.tile([P, 2, 4, N], BF16)
+        q_view = q_prev.rearrange("(c t p) k -> c p t k", c=2, t=4, p=P)
+        for c in range(2):
+            nc.sync.dma_start(out=raw_q[:, c], in_=q_view[c])
+        x_sb = keep.tile([P, 8, N], BF16)
+        x_view = x.rearrange("(p b) k -> p b k", b=8)
+        for j in range(4):
+            nc.sync.dma_start(out=x_sb[:, 2 * j : 2 * j + 2, :], in_=x_view[:, 2 * j : 2 * j + 2, :])
+        out_view = out.rearrange("(p b) i -> p b i", b=8)
+
+        ident = const.tile([P, P], F32)
+        make_identity(nc, ident[:])
+        dmask = const.tile([P, 4, P, 4], BF16)
+        nc.vector.memset(dmask[:], 0.0)
+        for r in range(4):
+            nc.vector.tensor_copy(out=dmask[:, r, :, r], in_=ident[:])
+
+        s_ps = psum_s.tile([P, 1], F32)
+        for m in range(8):
+            nc.tensor.matmul(
+                out=s_ps[:],
+                lhsT=vcol[:, m : m + 1].to_broadcast([P, P]),
+                rhs=vcol[:, m : m + 1],
+                start=(m == 0),
+                stop=(m == 7),
+            )
+        half = const.tile([P, 1], F32)
+        nc.vector.tensor_scalar(out=half[:], in0=s_ps[:], scalar1=-0.5, scalar2=None, op0=MULT)
+        c2 = const.tile([P, 1], F32)
+        nc.vector.reciprocal(out=c2[:], in_=half[:])
+
+        h_in = keep.tile([P, 2, N, 4], BF16, align_bytes=64)
+        h_codes = keep.tile([P, 2, N], U32, align_bytes=64)
+        h_scales = keep.tile([P, 2, N], U8, align_bytes=64)
+        q_in = keep.tile([P, 2, N, 4], BF16, align_bytes=64)
+        q_codes = keep.tile([P, 2, N], U32, align_bytes=64)
+        q_scales = keep.tile([P, 2, N], U8, align_bytes=64)
+        x_in = keep.tile([P, 8, N], BF16, align_bytes=64)
+        x_codes = keep.tile([P, 8, 2, P], U32, align_bytes=64)
+        x_scales = keep.tile([P, 8, 2, P], U8, align_bytes=64)
+        w_in = keep.tile([P, 2, N, 4], BF16, align_bytes=64)
+        w_codes = keep.tile([P, 2, N], U32, align_bytes=64)
+        w_scales = keep.tile([P, 2, N], U8, align_bytes=64)
+
+        def form_h(c, ib):
+            hb = psum_a.tile([P, 4, P], F32, tag="hw")
+            for t in range(4):
+                jb = 4 * c + t
+                nc.tensor.matmul(
+                    out=hb[:, t, :],
+                    lhsT=vrow[:, jb * P : (jb + 1) * P],
+                    rhs=vrow[:, ib * P : (ib + 1) * P],
+                    start=True,
+                    stop=True,
+                )
+            dst = h_in[:, c, ib * P : (ib + 1) * P, :]
+            src = hb[:].rearrange("p t i -> p i t")
+            r = ib - 4 * c
+            if 0 <= r < 4:
+                nc.vector.scalar_tensor_tensor(
+                    out=dst, in0=src, scalar=c2[:, 0:1], in1=dmask[:, r], op0=MULT, op1=ADD
+                )
+            else:
+                nc.scalar.activation(out=dst, in_=src, func=COPY, scale=c2[:, 0:1])
+
+        def quantise(src, codes, scales):
+            nc.vector.quantize_mx(out=codes.bitcast(FP8X4), scales=scales, in_=src)
+
+        def quantise_h(c, ih):
+            cols = slice(512 * ih, 512 * ih + 512)
+            quantise(
+                h_in[:, c, cols, :].rearrange("p i t -> p (i t)"), h_codes[:, c, cols], h_scales[:, c, cols]
+            )
+
+        def regroup_q(c, g):
+            for u in range(2):
+                cols = slice(512 * g + 256 * u, 512 * g + 256 * u + 256)
+                nc.vector.tensor_copy(
+                    out=q_in[:, c, cols, :].rearrange("p (e k) t -> p e k t", e=2),
+                    in_=raw_q[:, c, :, cols].rearrange("p t (k e) -> p e k t", e=2),
+                )
+
+        def quantise_q(c, g):
+            cols = slice(512 * g, 512 * g + 512)
+            quantise(
+                q_in[:, c, cols, :].rearrange("p k t -> p (k t)"), q_codes[:, c, cols], q_scales[:, c, cols]
+            )
+
+        def transpose_x(bt):
+            xt = psum_b.tile([P, 4, P], F32, tag="xo")
+            words = x_sb[:, bt, :].bitcast(F32)
+            for gu in range(4):
+                nc.tensor.transpose(xt[:, gu, :], words[:, gu * P : (gu + 1) * P], ident[:])
+            nc.scalar.copy(
+                out=x_in[:, bt, :].bitcast(F32).rearrange("p (g b u) -> p g b u", g=2, u=2),
+                in_=xt[:].rearrange("p (g u) b -> p g b u", g=2),
+            )
+
+        def quantise_x(j):
+            quantise(
+                x_in[:, 2 * j : 2 * j + 2, :].rearrange("p b k -> p (b k)"),
+                x_codes[:, 2 * j : 2 * j + 2].rearrange("p b g m -> p (b g m)"),
+                x_scales[:, 2 * j : 2 * j + 2].rearrange("p b g m -> p (b g m)"),
+            )
+
+        def make_w(g, ib):
+            wb = psum_a.tile([P, 4, P], F32, tag="hw")
+            for t in range(4):
+                kcols = slice(512 * g + P * t, 512 * g + P * t + P)
+                icols = slice(ib * P, (ib + 1) * P)
+                for c in range(2):
+                    nc.tensor.matmul_mx(
+                        out=wb[:, t, :],
+                        lhsT=q_codes[:, c, kcols].bitcast(FP8X4),
+                        lhsT_scale=q_scales[:, c, kcols],
+                        rhs=h_codes[:, c, icols].bitcast(FP8X4),
+                        rhs_scale=h_scales[:, c, icols],
+                        start=(c == 0),
+                        stop=(c == 1),
+                    )
+            nc.scalar.copy(
+                out=w_in[:, g, ib * P : (ib + 1) * P, :], in_=wb[:].rearrange("p t i -> p i t")
+            )
+
+        def quantise_w(g, ih):
+            cols = slice(512 * ih, 512 * ih + 512)
+            quantise(
+                w_in[:, g, cols, :].rearrange("p i t -> p (i t)"), w_codes[:, g, cols], w_scales[:, g, cols]
+            )
+
+        def make_out(bt):
+            o_sb = stage.tile([P, N], F32)
+            for ih in range(2):
+                cols = slice(512 * ih, 512 * ih + 512)
+                ob = psum_b.tile([P, 512], F32, tag="xo")
+                for g in range(2):
+                    nc.tensor.matmul_mx(
+                        out=ob[:],
+                        lhsT=x_codes[:, bt, g, :].bitcast(FP8X4),
+                        lhsT_scale=x_scales[:, bt, g, :],
+                        rhs=w_codes[:, g, cols].bitcast(FP8X4),
+                        rhs_scale=w_scales[:, g, cols],
+                        start=(g == 0),
+                        stop=(g == 1),
+                    )
+                if ih == 0:
+                    nc.vector.tensor_copy(out=o_sb[:, cols], in_=ob[:])
+                else:
+                    nc.scalar.copy(out=o_sb[:, cols], in_=ob[:])
+            nc.sync.dma_start(out=out_view[:, bt, :], in_=o_sb[:])
+
+        for ib in range(4):
+            for c in range(2):
+                form_h(c, ib)
+        regroup_q(0, 0)
+        quantise_h(0, 0)
+        regroup_q(1, 0)
+        quantise_h(1, 0)
+        quantise_q(0, 0)
+        quantise_q(1, 0)
+        for bt in range(8):
+            transpose_x(bt)
+        for ib in range(4):
+            make_w(0, ib)
+        regroup_q(0, 1)
+        regroup_q(1, 1)
+        quantise_q(0, 1)
+        quantise_q(1, 1)
+        for ib in range(4):
+            make_w(1, ib)
+        for ib in range(4, 8):
+            for c in range(2):
+                form_h(c, ib)
+        quantise_h(0, 1)
+        quantise_h(1, 1)
+        quantise_w(0, 0)
+        quantise_w(1, 0)
+        for g in range(2):
+            for ib in range(4, 8):
+                make_w(g, ib)
+        for j in range(4):
+            quantise_x(j)
+        quantise_w(0, 1)
+        quantise_w(1, 1)
+        for bt in range(8):
+            make_out(bt)

@@ -17,16 +17,175 @@ COPY = mybir.ActivationFunctionType.Copy
 P = 128
 N = 1024
 
+PROGRAM = [
+    ("S8", 0),
+    ("QR", 0, 0, 0, "V"),
+    ("HP", 1, 0, 1),
+    ("C2",),
+    ("HP", 0, 0, 2),
+    ("QR", 0, 0, 1, "V"),
+    ("HC", 1, 0, "S"),
+    ("HP", 1, 1, 3),
+    ("QR", 1, 0, 0, "V"),
+    ("HP", 0, 1, 4),
+    ("HC", 1, 1, "S"),
+    ("HP", 1, 2, 5),
+    ("HC", 0, 0, "V"),
+    ("XT", 0, 6),
+    ("HC", 1, 2, "S"),
+    ("HC", 0, 1, "V"),
+    ("XT", 1, 7),
+    ("HP", 0, 2, 0),
+    ("QR", 1, 0, 1, "V"),
+    ("XC", 0, "S"),
+    ("XT", 2, 1),
+    ("XC", 1, "S"),
+    ("QH", 0, 0, 0),
+    ("XT", 3, 3),
+    ("QH", 1, 0, 0),
+    ("HP", 1, 3, 2),
+    ("XC", 2, "S"),
+    ("QQ", 0, 0),
+    ("HP", 0, 3, 4),
+    ("HC", 1, 3, "S"),
+    ("HP", 0, 4, 5),
+    ("QQ", 1, 0),
+    ("HP", 1, 4, 6),
+    ("HP", 0, 5, 7),
+    ("HC", 0, 4, "S"),
+    ("HC", 0, 2, "V"),
+    ("HP", 1, 5, 1),
+    ("W", 0, 0, 2),
+    ("HC", 0, 5, "S"),
+    ("HC", 0, 3, "V"),
+    ("W", 0, 1, 5),
+    ("XC", 3, "S"),
+    ("QH", 0, 0, 1),
+    ("QH", 1, 0, 1),
+    ("HP", 0, 6, 0),
+    ("WC", 0, 0, "S"),
+    ("HC", 1, 4, "V"),
+    ("HP", 1, 6, 7),
+    ("HC", 0, 6, "S"),
+    ("W", 0, 2, 4),
+    ("HC", 1, 5, "V"),
+    ("QR", 1, 1, 0, "S"),
+    ("W", 0, 3, 3),
+    ("QH", 0, 1, 0),
+    ("QH", 1, 1, 0),
+    ("HC", 1, 6, "V"),
+    ("HP", 0, 7, 2),
+    ("W", 0, 4, 6),
+    ("QR", 0, 1, 0, "V"),
+    ("HC", 0, 7, "S"),
+    ("W", 0, 5, 0),
+    ("QR", 0, 1, 1, "V"),
+    ("QR", 1, 1, 1, "S"),
+    ("HP", 1, 7, 1),
+    ("XT", 4, 7),
+    ("QH", 0, 1, 1),
+    ("HC", 1, 7, "V"),
+    ("XT", 5, 2),
+    ("WC", 0, 1, "S"),
+    ("QH", 1, 1, 1),
+    ("XT", 6, 1),
+    ("QQ", 0, 1),
+    ("WC", 0, 2, "S"),
+    ("XT", 7, 5),
+    ("WC", 0, 3, "S"),
+    ("QQ", 1, 1),
+    ("W", 0, 6, 4),
+    ("WC", 0, 4, "S"),
+    ("QX", 0),
+    ("W", 0, 7, 3),
+    ("WC", 0, 5, "S"),
+    ("QW", 0, 0),
+    ("W", 1, 0, 6),
+    ("WC", 0, 6, "S"),
+    ("QX", 1),
+    ("W", 1, 1, 0),
+    ("WC", 0, 7, "S"),
+    ("XC", 4, "V"),
+    ("W", 1, 2, 4),
+    ("WC", 1, 0, "S"),
+    ("XC", 5, "V"),
+    ("W", 1, 3, 3),
+    ("WC", 1, 1, "S"),
+    ("QX", 2),
+    ("WC", 1, 2, "S"),
+    ("W", 1, 4, 7),
+    ("XC", 6, "V"),
+    ("WC", 1, 3, "S"),
+    ("W", 1, 5, 6),
+    ("XC", 7, "V"),
+    ("WC", 1, 4, "S"),
+    ("QW", 1, 0),
+    ("W", 1, 6, 2),
+    ("WC", 1, 5, "S"),
+    ("QX", 3),
+    ("W", 1, 7, 0),
+    ("WC", 1, 6, "S"),
+    ("QW", 0, 1),
+    ("O", 0, 0, 4),
+    ("WC", 1, 7, "S"),
+    ("O", 1, 0, 1),
+    ("OC", 0, 0, "V"),
+    ("O", 2, 0, 3),
+    ("OC", 1, 0, "S"),
+    ("QW", 1, 1),
+    ("ST", 0, 0),
+    ("O", 3, 0, 5),
+    ("OC", 2, 0, "V"),
+    ("ST", 1, 0),
+    ("O", 4, 0, 7),
+    ("OC", 3, 0, "S"),
+    ("ST", 2, 0),
+    ("O", 5, 0, 6),
+    ("OC", 4, 0, "V"),
+    ("ST", 3, 0),
+    ("O", 6, 0, 2),
+    ("OC", 5, 0, "S"),
+    ("ST", 4, 0),
+    ("O", 7, 0, 0),
+    ("OC", 6, 0, "V"),
+    ("ST", 5, 0),
+    ("O", 0, 1, 4),
+    ("OC", 7, 0, "S"),
+    ("ST", 6, 0),
+    ("O", 1, 1, 1),
+    ("OC", 0, 1, "S"),
+    ("ST", 7, 0),
+    ("O", 2, 1, 3),
+    ("OC", 1, 1, "V"),
+    ("O", 3, 1, 5),
+    ("ST", 0, 1),
+    ("OC", 2, 1, "S"),
+    ("O", 4, 1, 7),
+    ("ST", 1, 1),
+    ("OC", 3, 1, "V"),
+    ("O", 5, 1, 6),
+    ("ST", 2, 1),
+    ("OC", 4, 1, "S"),
+    ("O", 6, 1, 2),
+    ("ST", 3, 1),
+    ("OC", 5, 1, "V"),
+    ("O", 7, 1, 0),
+    ("ST", 4, 1),
+    ("OC", 6, 1, "S"),
+    ("ST", 5, 1),
+    ("OC", 7, 1, "V"),
+    ("ST", 6, 1),
+    ("ST", 7, 1),
+]
+
 
 def tile_householderlinear_pa_kernel(tc, x, q_prev, v, out):
     nc = tc.nc
     with ExitStack() as ctx:
+        ctx.enter_context(tc.manual_schedule())
         const = ctx.enter_context(tc.tile_pool(name="const", bufs=1))
         keep = ctx.enter_context(tc.tile_pool(name="keep", bufs=1))
-        stage = ctx.enter_context(tc.tile_pool(name="stage", bufs=3))
-        psum_a = ctx.enter_context(tc.psum_pool(name="psum_a", bufs=4))
-        psum_b = ctx.enter_context(tc.psum_pool(name="psum_b", bufs=3))
-        psum_s = ctx.enter_context(tc.psum_pool(name="psum_s", bufs=1))
+        psum = ctx.enter_context(tc.psum_pool(name="psum", bufs=1))
 
         vcol = const.tile([P, 8], BF16)
         nc.scalar.dma_start(out=vcol[:], in_=v.rearrange("(p m) -> p m", m=8))
@@ -36,13 +195,25 @@ def tile_householderlinear_pa_kernel(tc, x, q_prev, v, out):
 
         raw_q = keep.tile([P, 2, 4, N], BF16)
         q_view = q_prev.rearrange("(c t p) k -> c p t k", c=2, t=4, p=P)
-        for c in range(2):
-            nc.sync.dma_start(out=raw_q[:, c], in_=q_view[c])
         x_sb = keep.tile([P, 8, N], BF16)
         x_view = x.rearrange("(p b) k -> p b k", b=8)
-        for j in range(4):
-            nc.sync.dma_start(out=x_sb[:, 2 * j : 2 * j + 2, :], in_=x_view[:, 2 * j : 2 * j + 2, :])
         out_view = out.rearrange("(p b) i -> p b i", b=8)
+
+        def load_q(c, g):
+            cols = slice(512 * g, 512 * g + 512)
+            nc.sync.dma_start(out=raw_q[:, c, :, cols], in_=q_view[c][:, :, cols])
+
+        def load_x(j):
+            nc.sync.dma_start(out=x_sb[:, 2 * j : 2 * j + 2, :], in_=x_view[:, 2 * j : 2 * j + 2, :])
+
+        load_q(0, 0)
+        load_q(1, 0)
+        load_x(0)
+        load_x(1)
+        load_x(2)
+        load_x(3)
+        load_q(0, 1)
+        load_q(1, 1)
 
         ident = const.tile([P, P], F32)
         make_identity(nc, ident[:])
@@ -50,20 +221,8 @@ def tile_householderlinear_pa_kernel(tc, x, q_prev, v, out):
         nc.vector.memset(dmask[:], 0.0)
         for r in range(4):
             nc.vector.tensor_copy(out=dmask[:, r, :, r], in_=ident[:])
-
-        s_ps = psum_s.tile([P, 1], F32)
-        for m in range(8):
-            nc.tensor.matmul(
-                out=s_ps[:],
-                lhsT=vcol[:, m : m + 1].to_broadcast([P, P]),
-                rhs=vcol[:, m : m + 1],
-                start=(m == 0),
-                stop=(m == 7),
-            )
         half = const.tile([P, 1], F32)
-        nc.vector.tensor_scalar(out=half[:], in0=s_ps[:], scalar1=-0.5, scalar2=None, op0=MULT)
         c2 = const.tile([P, 1], F32)
-        nc.vector.reciprocal(out=c2[:], in_=half[:])
 
         h_in = keep.tile([P, 2, N, 4], BF16, align_bytes=64)
         h_codes = keep.tile([P, 2, N], U32, align_bytes=64)
@@ -77,98 +236,137 @@ def tile_householderlinear_pa_kernel(tc, x, q_prev, v, out):
         w_in = keep.tile([P, 2, N, 4], BF16, align_bytes=64)
         w_codes = keep.tile([P, 2, N], U32, align_bytes=64)
         w_scales = keep.tile([P, 2, N], U8, align_bytes=64)
+        o_all = keep.tile([P, 8, N], F32)
 
-        def form_h(c, ib):
-            hb = psum_a.tile([P, 4, P], F32, tag="hw")
-            for t in range(4):
-                jb = 4 * c + t
-                nc.tensor.matmul(
-                    out=hb[:, t, :],
-                    lhsT=vrow[:, jb * P : (jb + 1) * P],
-                    rhs=vrow[:, ib * P : (ib + 1) * P],
-                    start=True,
-                    stop=True,
-                )
-            dst = h_in[:, c, ib * P : (ib + 1) * P, :]
-            src = hb[:].rearrange("p t i -> p i t")
-            r = ib - 4 * c
-            if 0 <= r < 4:
-                nc.vector.scalar_tensor_tensor(
-                    out=dst, in0=src, scalar=c2[:, 0:1], in1=dmask[:, r], op0=MULT, op1=ADD
-                )
+        banks = {}
+
+        def bank(key, k, shape):
+            t = psum.tile(shape, F32, tag="bank%d" % k, name="ps%s%d" % (key[0], len(banks)))
+            banks[key] = t
+            return t
+
+        def copy_on(eng, dst, src):
+            if eng == "V":
+                nc.vector.tensor_copy(out=dst, in_=src)
             else:
-                nc.scalar.activation(out=dst, in_=src, func=COPY, scale=c2[:, 0:1])
+                nc.scalar.copy(out=dst, in_=src)
 
         def quantise(src, codes, scales):
             nc.vector.quantize_mx(out=codes.bitcast(FP8X4), scales=scales, in_=src)
 
-        def quantise_h(c, ih):
-            cols = slice(512 * ih, 512 * ih + 512)
-            quantise(
-                h_in[:, c, cols, :].rearrange("p i t -> p (i t)"), h_codes[:, c, cols], h_scales[:, c, cols]
-            )
-
-        def regroup_q(c, g):
-            for u in range(2):
-                cols = slice(512 * g + 256 * u, 512 * g + 256 * u + 256)
-                nc.vector.tensor_copy(
-                    out=q_in[:, c, cols, :].rearrange("p (e k) t -> p e k t", e=2),
-                    in_=raw_q[:, c, :, cols].rearrange("p t (k e) -> p e k t", e=2),
-                )
-
-        def quantise_q(c, g):
-            cols = slice(512 * g, 512 * g + 512)
-            quantise(
-                q_in[:, c, cols, :].rearrange("p k t -> p (k t)"), q_codes[:, c, cols], q_scales[:, c, cols]
-            )
-
-        def transpose_x(bt):
-            xt = psum_b.tile([P, 4, P], F32, tag="xo")
-            words = x_sb[:, bt, :].bitcast(F32)
-            for gu in range(4):
-                nc.tensor.transpose(xt[:, gu, :], words[:, gu * P : (gu + 1) * P], ident[:])
-            nc.scalar.copy(
-                out=x_in[:, bt, :].bitcast(F32).rearrange("p (g b u) -> p g b u", g=2, u=2),
-                in_=xt[:].rearrange("p (g u) b -> p g b u", g=2),
-            )
-
-        def quantise_x(j):
-            quantise(
-                x_in[:, 2 * j : 2 * j + 2, :].rearrange("p b k -> p (b k)"),
-                x_codes[:, 2 * j : 2 * j + 2].rearrange("p b g m -> p (b g m)"),
-                x_scales[:, 2 * j : 2 * j + 2].rearrange("p b g m -> p (b g m)"),
-            )
-
-        def make_w(g, ib):
-            wb = psum_a.tile([P, 4, P], F32, tag="hw")
-            for t in range(4):
-                kcols = slice(512 * g + P * t, 512 * g + P * t + P)
-                icols = slice(ib * P, (ib + 1) * P)
-                for c in range(2):
-                    nc.tensor.matmul_mx(
-                        out=wb[:, t, :],
-                        lhsT=q_codes[:, c, kcols].bitcast(FP8X4),
-                        lhsT_scale=q_scales[:, c, kcols],
-                        rhs=h_codes[:, c, icols].bitcast(FP8X4),
-                        rhs_scale=h_scales[:, c, icols],
-                        start=(c == 0),
-                        stop=(c == 1),
+        for op in PROGRAM:
+            kind = op[0]
+            if kind == "S8":
+                s_ps = bank(("S",), op[1], [P, 1])
+                for m in range(8):
+                    nc.tensor.matmul(
+                        out=s_ps[:],
+                        lhsT=vcol[:, m : m + 1].to_broadcast([P, P]),
+                        rhs=vcol[:, m : m + 1],
+                        start=(m == 0),
+                        stop=(m == 7),
                     )
-            nc.scalar.copy(
-                out=w_in[:, g, ib * P : (ib + 1) * P, :], in_=wb[:].rearrange("p t i -> p i t")
-            )
-
-        def quantise_w(g, ih):
-            cols = slice(512 * ih, 512 * ih + 512)
-            quantise(
-                w_in[:, g, cols, :].rearrange("p i t -> p (i t)"), w_codes[:, g, cols], w_scales[:, g, cols]
-            )
-
-        def make_out(bt):
-            o_sb = stage.tile([P, N], F32)
-            for ih in range(2):
+            elif kind == "C2":
+                nc.vector.tensor_scalar(out=half[:], in0=banks[("S",)][:], scalar1=-0.5, scalar2=None, op0=MULT)
+                nc.vector.reciprocal(out=c2[:], in_=half[:])
+            elif kind == "HP":
+                c, ib = op[1], op[2]
+                hb = bank(("H", c, ib), op[3], [P, 4, P])
+                for t in range(4):
+                    jb = 4 * c + t
+                    nc.tensor.matmul(
+                        out=hb[:, t, :],
+                        lhsT=vrow[:, jb * P : (jb + 1) * P],
+                        rhs=vrow[:, ib * P : (ib + 1) * P],
+                        start=True,
+                        stop=True,
+                    )
+            elif kind == "HC":
+                c, ib = op[1], op[2]
+                dst = h_in[:, c, ib * P : (ib + 1) * P, :]
+                src = banks[("H", c, ib)][:].rearrange("p t i -> p i t")
+                r = ib - 4 * c
+                if 0 <= r < 4:
+                    nc.vector.scalar_tensor_tensor(
+                        out=dst, in0=src, scalar=c2[:, 0:1], in1=dmask[:, r], op0=MULT, op1=ADD
+                    )
+                elif op[3] == "V":
+                    nc.vector.tensor_scalar(out=dst, in0=src, scalar1=c2[:, 0:1], scalar2=None, op0=MULT)
+                else:
+                    nc.scalar.activation(out=dst, in_=src, func=COPY, scale=c2[:, 0:1])
+            elif kind == "QH":
+                c = op[1]
+                cols = slice(512 * op[2] + 256 * op[3], 512 * op[2] + 256 * op[3] + 256)
+                quantise(
+                    h_in[:, c, cols, :].rearrange("p i t -> p (i t)"), h_codes[:, c, cols], h_scales[:, c, cols]
+                )
+            elif kind == "QR":
+                c, g, u = op[1], op[2], op[3]
+                cols = slice(512 * g + 256 * u, 512 * g + 256 * u + 256)
+                copy_on(
+                    op[4],
+                    q_in[:, c, cols, :].rearrange("p (e k) t -> p e k t", e=2),
+                    raw_q[:, c, :, cols].rearrange("p t (k e) -> p e k t", e=2),
+                )
+            elif kind == "QQ":
+                c = op[1]
+                cols = slice(512 * op[2], 512 * op[2] + 512)
+                quantise(
+                    q_in[:, c, cols, :].rearrange("p k t -> p (k t)"), q_codes[:, c, cols], q_scales[:, c, cols]
+                )
+            elif kind == "XT":
+                bt = op[1]
+                xt = bank(("X", bt), op[2], [P, 4, P])
+                words = x_sb[:, bt, :].bitcast(F32)
+                for gu in range(4):
+                    nc.tensor.transpose(xt[:, gu, :], words[:, gu * P : (gu + 1) * P], ident[:])
+            elif kind == "XC":
+                bt = op[1]
+                copy_on(
+                    op[2],
+                    x_in[:, bt, :].bitcast(F32).rearrange("p (g b u) -> p g b u", g=2, u=2),
+                    banks[("X", bt)][:].rearrange("p (g u) b -> p g b u", g=2),
+                )
+            elif kind == "QX":
+                j = op[1]
+                quantise(
+                    x_in[:, 2 * j : 2 * j + 2, :].rearrange("p b k -> p (b k)"),
+                    x_codes[:, 2 * j : 2 * j + 2].rearrange("p b g m -> p (b g m)"),
+                    x_scales[:, 2 * j : 2 * j + 2].rearrange("p b g m -> p (b g m)"),
+                )
+            elif kind == "W":
+                g, ib = op[1], op[2]
+                wb = bank(("W", g, ib), op[3], [P, 4, P])
+                icols = slice(ib * P, (ib + 1) * P)
+                for t in range(4):
+                    kcols = slice(512 * g + P * t, 512 * g + P * t + P)
+                    for c in range(2):
+                        nc.tensor.matmul_mx(
+                            out=wb[:, t, :],
+                            lhsT=q_codes[:, c, kcols].bitcast(FP8X4),
+                            lhsT_scale=q_scales[:, c, kcols],
+                            rhs=h_codes[:, c, icols].bitcast(FP8X4),
+                            rhs_scale=h_scales[:, c, icols],
+                            start=(c == 0),
+                            stop=(c == 1),
+                        )
+            elif kind == "WC":
+                g, ib = op[1], op[2]
+                copy_on(
+                    op[3],
+                    w_in[:, g, ib * P : (ib + 1) * P, :],
+                    banks[("W", g, ib)][:].rearrange("p t i -> p i t"),
+                )
+            elif kind == "QW":
+                g = op[1]
+                cols = slice(512 * op[2], 512 * op[2] + 512)
+                quantise(
+                    w_in[:, g, cols, :].rearrange("p i t -> p (i t)"), w_codes[:, g, cols], w_scales[:, g, cols]
+                )
+            elif kind == "O":
+                bt, ih = op[1], op[2]
+                ob = bank(("O", bt, ih), op[3], [P, 512])
                 cols = slice(512 * ih, 512 * ih + 512)
-                ob = psum_b.tile([P, 512], F32, tag="xo")
                 for g in range(2):
                     nc.tensor.matmul_mx(
                         out=ob[:],
@@ -179,44 +377,12 @@ def tile_householderlinear_pa_kernel(tc, x, q_prev, v, out):
                         start=(g == 0),
                         stop=(g == 1),
                     )
-                if ih == 0:
-                    nc.vector.tensor_copy(out=o_sb[:, cols], in_=ob[:])
-                else:
-                    nc.scalar.copy(out=o_sb[:, cols], in_=ob[:])
-            nc.sync.dma_start(out=out_view[:, bt, :], in_=o_sb[:])
-
-        for ib in range(4):
-            for c in range(2):
-                form_h(c, ib)
-        regroup_q(0, 0)
-        quantise_h(0, 0)
-        regroup_q(1, 0)
-        quantise_h(1, 0)
-        quantise_q(0, 0)
-        quantise_q(1, 0)
-        for bt in range(8):
-            transpose_x(bt)
-        for ib in range(4):
-            make_w(0, ib)
-        regroup_q(0, 1)
-        regroup_q(1, 1)
-        quantise_q(0, 1)
-        quantise_q(1, 1)
-        for ib in range(4):
-            make_w(1, ib)
-        for ib in range(4, 8):
-            for c in range(2):
-                form_h(c, ib)
-        quantise_h(0, 1)
-        quantise_h(1, 1)
-        quantise_w(0, 0)
-        quantise_w(1, 0)
-        for g in range(2):
-            for ib in range(4, 8):
-                make_w(g, ib)
-        for j in range(4):
-            quantise_x(j)
-        quantise_w(0, 1)
-        quantise_w(1, 1)
-        for bt in range(8):
-            make_out(bt)
+            elif kind == "OC":
+                bt, ih = op[1], op[2]
+                copy_on(op[3], o_all[:, bt, 512 * ih : 512 * ih + 512], banks[("O", bt, ih)][:])
+            elif kind == "ST":
+                bt, ih = op[1], op[2]
+                cols = slice(512 * ih, 512 * ih + 512)
+                nc.sync.dma_start(out=out_view[:, bt, cols], in_=o_all[:, bt, cols])
+            else:
+                assert False, kind

@@ -9,6 +9,7 @@ F32 = mybir.dt.float32
 BF16 = mybir.dt.bfloat16
 U32 = mybir.dt.uint32
 U8 = mybir.dt.uint8
+I32 = mybir.dt.int32
 FP8X4 = mybir.dt.float8_e4m3fn_x4
 MULT = mybir.AluOpType.mult
 ADD = mybir.AluOpType.add
@@ -18,158 +19,158 @@ P = 128
 N = 1024
 
 PROGRAM = [
-    ("S8", 0),
     ("QR", 0, 0, 0, "V"),
+    ("S8", 0),
+    ("QR", 0, 0, 1, "V"),
+    ("QR", 1, 0, 0, "V"),
     ("HP", 1, 0, 1),
     ("C2",),
     ("HP", 0, 0, 2),
-    ("QR", 0, 0, 1, "V"),
-    ("HC", 1, 0, "S"),
-    ("HP", 1, 1, 3),
-    ("QR", 1, 0, 0, "V"),
-    ("HP", 0, 1, 4),
-    ("HC", 1, 1, "S"),
-    ("HP", 1, 2, 5),
-    ("HC", 0, 0, "V"),
-    ("XT", 0, 6),
-    ("HC", 1, 2, "S"),
-    ("HC", 0, 1, "V"),
-    ("XT", 1, 7),
-    ("HP", 0, 2, 0),
     ("QR", 1, 0, 1, "V"),
-    ("XC", 0, "S"),
-    ("XT", 2, 1),
-    ("XC", 1, "S"),
-    ("QH", 0, 0, 0),
-    ("XT", 3, 3),
-    ("QH", 1, 0, 0),
-    ("HP", 1, 3, 2),
-    ("XC", 2, "S"),
+    ("HC", 1, 0, "S"),
+    ("XT", 0, 3),
+    ("HC", 0, 0, "V"),
+    ("XT", 1, 4),
     ("QQ", 0, 0),
-    ("HP", 0, 3, 4),
-    ("HC", 1, 3, "S"),
-    ("HP", 0, 4, 5),
+    ("XC", 0, "S"),
+    ("XT", 2, 5),
     ("QQ", 1, 0),
-    ("HP", 1, 4, 6),
-    ("HP", 0, 5, 7),
-    ("HC", 0, 4, "S"),
-    ("HC", 0, 2, "V"),
-    ("HP", 1, 5, 1),
-    ("W", 0, 0, 2),
-    ("HC", 0, 5, "S"),
-    ("HC", 0, 3, "V"),
-    ("W", 0, 1, 5),
-    ("XC", 3, "S"),
-    ("QH", 0, 0, 1),
-    ("QH", 1, 0, 1),
-    ("HP", 0, 6, 0),
-    ("WC", 0, 0, "S"),
-    ("HC", 1, 4, "V"),
-    ("HP", 1, 6, 7),
-    ("HC", 0, 6, "S"),
-    ("W", 0, 2, 4),
-    ("HC", 1, 5, "V"),
-    ("QR", 1, 1, 0, "S"),
-    ("W", 0, 3, 3),
-    ("QH", 0, 1, 0),
-    ("QH", 1, 1, 0),
-    ("HC", 1, 6, "V"),
-    ("HP", 0, 7, 2),
-    ("W", 0, 4, 6),
+    ("XT", 3, 6),
+    ("XC", 1, "S"),
+    ("HP", 1, 1, 7),
     ("QR", 0, 1, 0, "V"),
-    ("HC", 0, 7, "S"),
-    ("W", 0, 5, 0),
+    ("XC", 2, "S"),
+    ("HP", 0, 1, 0),
+    ("HP", 1, 2, 1),
+    ("HC", 1, 1, "S"),
+    ("HC", 0, 1, "V"),
+    ("HP", 0, 2, 2),
+    ("HP", 1, 3, 3),
+    ("QH", 0, 0, 0),
+    ("HP", 0, 3, 4),
+    ("HC", 1, 2, "S"),
+    ("QH", 1, 0, 0),
+    ("HP", 0, 4, 5),
+    ("HC", 0, 2, "V"),
+    ("HP", 1, 4, 0),
+    ("HC", 1, 3, "S"),
+    ("W", 0, 0, 7),
+    ("HC", 0, 3, "V"),
+    ("HC", 0, 4, "S"),
+    ("W", 0, 1, 1),
+    ("QH", 0, 0, 1),
+    ("XC", 3, "S"),
+    ("QH", 1, 0, 1),
+    ("HP", 0, 5, 2),
+    ("HC", 1, 4, "V"),
+    ("HP", 1, 5, 3),
+    ("WC", 0, 0, "S"),
+    ("W", 0, 2, 4),
     ("QR", 0, 1, 1, "V"),
-    ("QR", 1, 1, 1, "S"),
-    ("HP", 1, 7, 1),
-    ("XT", 4, 7),
-    ("QH", 0, 1, 1),
-    ("HC", 1, 7, "V"),
-    ("XT", 5, 2),
+    ("HC", 0, 5, "S"),
+    ("W", 0, 3, 5),
+    ("HC", 1, 5, "V"),
     ("WC", 0, 1, "S"),
-    ("QH", 1, 1, 1),
-    ("XT", 6, 1),
-    ("QQ", 0, 1),
+    ("HP", 0, 6, 6),
+    ("QH", 0, 1, 0),
     ("WC", 0, 2, "S"),
-    ("XT", 7, 5),
+    ("HP", 1, 6, 0),
+    ("QH", 1, 1, 0),
+    ("HP", 0, 7, 7),
+    ("QR", 1, 1, 0, "V"),
+    ("HC", 0, 6, "S"),
+    ("HP", 1, 7, 2),
+    ("W", 0, 4, 3),
+    ("HC", 1, 6, "V"),
+    ("HC", 0, 7, "S"),
+    ("W", 0, 5, 1),
+    ("HC", 1, 7, "V"),
     ("WC", 0, 3, "S"),
-    ("QQ", 1, 1),
-    ("W", 0, 6, 4),
+    ("XT", 4, 4),
+    ("QH", 0, 1, 1),
     ("WC", 0, 4, "S"),
-    ("QX", 0),
-    ("W", 0, 7, 3),
+    ("QH", 1, 1, 1),
+    ("XT", 5, 6),
+    ("QR", 1, 1, 1, "V"),
+    ("XT", 6, 0),
     ("WC", 0, 5, "S"),
-    ("QW", 0, 0),
-    ("W", 1, 0, 6),
+    ("XT", 7, 7),
+    ("QQ", 0, 1),
+    ("W", 0, 6, 2),
+    ("QQ", 1, 1),
+    ("W", 0, 7, 5),
     ("WC", 0, 6, "S"),
-    ("QX", 1),
-    ("W", 1, 1, 0),
+    ("QX", 0),
+    ("W", 1, 0, 3),
     ("WC", 0, 7, "S"),
-    ("XC", 4, "V"),
-    ("W", 1, 2, 4),
+    ("QW", 0, 0),
+    ("W", 1, 1, 1),
     ("WC", 1, 0, "S"),
-    ("XC", 5, "V"),
-    ("W", 1, 3, 3),
+    ("QX", 1),
+    ("W", 1, 2, 2),
     ("WC", 1, 1, "S"),
-    ("QX", 2),
+    ("XC", 4, "V"),
+    ("W", 1, 3, 5),
+    ("XC", 5, "V"),
     ("WC", 1, 2, "S"),
-    ("W", 1, 4, 7),
-    ("XC", 6, "V"),
+    ("W", 1, 4, 3),
+    ("QX", 2),
     ("WC", 1, 3, "S"),
-    ("W", 1, 5, 6),
-    ("XC", 7, "V"),
+    ("W", 1, 5, 1),
+    ("XC", 6, "V"),
     ("WC", 1, 4, "S"),
     ("QW", 1, 0),
-    ("W", 1, 6, 2),
+    ("W", 1, 6, 4),
     ("WC", 1, 5, "S"),
-    ("QX", 3),
-    ("W", 1, 7, 0),
+    ("XC", 7, "V"),
+    ("W", 1, 7, 6),
     ("WC", 1, 6, "S"),
-    ("QW", 0, 1),
-    ("O", 0, 0, 4),
+    ("QX", 3),
+    ("O", 0, 0, 2),
     ("WC", 1, 7, "S"),
-    ("O", 1, 0, 1),
-    ("OC", 0, 0, "V"),
-    ("O", 2, 0, 3),
-    ("OC", 1, 0, "S"),
+    ("QW", 0, 1),
+    ("O", 1, 0, 5),
     ("QW", 1, 1),
-    ("ST", 0, 0),
-    ("O", 3, 0, 5),
-    ("OC", 2, 0, "V"),
+    ("O", 2, 0, 0),
+    ("OC", 1, 0, "S"),
+    ("OC", 0, 0, "V"),
+    ("O", 3, 0, 3),
     ("ST", 1, 0),
-    ("O", 4, 0, 7),
+    ("OC", 2, 0, "V"),
+    ("O", 4, 0, 1),
     ("OC", 3, 0, "S"),
-    ("ST", 2, 0),
-    ("O", 5, 0, 6),
+    ("ST", 0, 0),
+    ("O", 5, 0, 7),
     ("OC", 4, 0, "V"),
-    ("ST", 3, 0),
-    ("O", 6, 0, 2),
+    ("ST", 2, 0),
+    ("O", 6, 0, 4),
     ("OC", 5, 0, "S"),
-    ("ST", 4, 0),
-    ("O", 7, 0, 0),
+    ("ST", 3, 0),
+    ("O", 7, 0, 6),
     ("OC", 6, 0, "V"),
-    ("ST", 5, 0),
-    ("O", 0, 1, 4),
+    ("ST", 4, 0),
+    ("O", 0, 1, 5),
     ("OC", 7, 0, "S"),
-    ("ST", 6, 0),
-    ("O", 1, 1, 1),
+    ("ST", 5, 0),
+    ("O", 1, 1, 2),
     ("OC", 0, 1, "S"),
-    ("ST", 7, 0),
-    ("O", 2, 1, 3),
+    ("ST", 6, 0),
+    ("O", 2, 1, 0),
     ("OC", 1, 1, "V"),
-    ("O", 3, 1, 5),
+    ("ST", 7, 0),
+    ("O", 3, 1, 3),
     ("ST", 0, 1),
     ("OC", 2, 1, "S"),
-    ("O", 4, 1, 7),
+    ("O", 4, 1, 1),
     ("ST", 1, 1),
     ("OC", 3, 1, "V"),
-    ("O", 5, 1, 6),
+    ("O", 5, 1, 7),
     ("ST", 2, 1),
     ("OC", 4, 1, "S"),
-    ("O", 6, 1, 2),
+    ("O", 6, 1, 4),
     ("ST", 3, 1),
     ("OC", 5, 1, "V"),
-    ("O", 7, 1, 0),
+    ("O", 7, 1, 6),
     ("ST", 4, 1),
     ("OC", 6, 1, "S"),
     ("ST", 5, 1),
@@ -188,12 +189,19 @@ def tile_householderlinear_pa_kernel(tc, x, q_prev, v, out):
         psum = ctx.enter_context(tc.psum_pool(name="psum", bufs=1))
 
         vcol = const.tile([P, 8], BF16)
-        nc.scalar.dma_start(out=vcol[:], in_=v.rearrange("(p m) -> p m", m=8))
+        nc.sync.dma_start(out=vcol[:], in_=v.rearrange("(p m) -> p m", m=8))
         vrow = const.tile([P, N], BF16)
-        nc.vector.memset(vrow[:], 0.0)
-        nc.scalar.dma_start(out=vrow[0:1, :], in_=v.rearrange("(o n) -> o n", o=1))
+        nc.vector.memset(vrow[:].bitcast(I32), 0)
+        nc.sync.dma_start(out=vrow[0:1, :], in_=v.rearrange("(o n) -> o n", o=1))
+        warm_in = const.tile([P, 1], F32)
+        warm_out = const.tile([P, 1], F32)
+        nc.gpsimd.memset(warm_in[:], 0.0)
+        nc.scalar.activation(out=warm_out[:], in_=warm_in[:], func=COPY)
 
-        raw_q = keep.tile([P, 2, 4, N], BF16)
+        raw_q = {}
+        for c in range(2):
+            for g in range(2):
+                raw_q[(c, g)] = keep.tile([P, 4, 512], BF16, name="raw_q%d%d" % (c, g))
         q_view = q_prev.rearrange("(c t p) k -> c p t k", c=2, t=4, p=P)
         x_sb = keep.tile([P, 8, N], BF16)
         x_view = x.rearrange("(p b) k -> p b k", b=8)
@@ -201,7 +209,7 @@ def tile_householderlinear_pa_kernel(tc, x, q_prev, v, out):
 
         def load_q(c, g):
             cols = slice(512 * g, 512 * g + 512)
-            nc.sync.dma_start(out=raw_q[:, c, :, cols], in_=q_view[c][:, :, cols])
+            nc.sync.dma_start(out=raw_q[(c, g)][:], in_=q_view[c][:, :, cols])
 
         def load_x(j):
             nc.sync.dma_start(out=x_sb[:, 2 * j : 2 * j + 2, :], in_=x_view[:, 2 * j : 2 * j + 2, :])
@@ -210,15 +218,15 @@ def tile_householderlinear_pa_kernel(tc, x, q_prev, v, out):
         load_q(1, 0)
         load_x(0)
         load_x(1)
-        load_x(2)
-        load_x(3)
         load_q(0, 1)
         load_q(1, 1)
+        load_x(2)
+        load_x(3)
 
         ident = const.tile([P, P], F32)
         make_identity(nc, ident[:])
         dmask = const.tile([P, 4, P, 4], BF16)
-        nc.vector.memset(dmask[:], 0.0)
+        nc.vector.memset(dmask[:].rearrange("p r i t -> p (r i t)").bitcast(I32), 0)
         for r in range(4):
             nc.vector.tensor_copy(out=dmask[:, r, :, r], in_=ident[:])
         half = const.tile([P, 1], F32)
@@ -306,7 +314,7 @@ def tile_householderlinear_pa_kernel(tc, x, q_prev, v, out):
                 copy_on(
                     op[4],
                     q_in[:, c, cols, :].rearrange("p (e k) t -> p e k t", e=2),
-                    raw_q[:, c, :, cols].rearrange("p t (k e) -> p e k t", e=2),
+                    raw_q[(c, g)][:, :, 256 * u : 256 * u + 256].rearrange("p t (k e) -> p e k t", e=2),
                 )
             elif kind == "QQ":
                 c = op[1]

@@ -17,167 +17,10 @@ COPY = mybir.ActivationFunctionType.Copy
 
 P = 128
 N = 1024
-
-PROGRAM = [
-    ("QR", 0, 0, 0, "V"),
-    ("S8", 0),
-    ("QR", 0, 0, 1, "V"),
-    ("QR", 1, 0, 0, "V"),
-    ("HP", 1, 0, 1),
-    ("C2",),
-    ("HP", 0, 0, 2),
-    ("QR", 1, 0, 1, "V"),
-    ("HC", 1, 0, "S"),
-    ("XT", 0, 3),
-    ("HC", 0, 0, "V"),
-    ("XT", 1, 4),
-    ("QQ", 0, 0),
-    ("XC", 0, "S"),
-    ("XT", 2, 5),
-    ("QQ", 1, 0),
-    ("XT", 3, 6),
-    ("XC", 1, "S"),
-    ("HP", 1, 1, 7),
-    ("QR", 0, 1, 0, "V"),
-    ("XC", 2, "S"),
-    ("HP", 0, 1, 0),
-    ("HP", 1, 2, 1),
-    ("HC", 1, 1, "S"),
-    ("HC", 0, 1, "V"),
-    ("HP", 0, 2, 2),
-    ("HP", 1, 3, 3),
-    ("QH", 0, 0, 0),
-    ("HP", 0, 3, 4),
-    ("HC", 1, 2, "S"),
-    ("QH", 1, 0, 0),
-    ("HP", 0, 4, 5),
-    ("HC", 0, 2, "V"),
-    ("HP", 1, 4, 0),
-    ("HC", 1, 3, "S"),
-    ("W", 0, 0, 7),
-    ("HC", 0, 3, "V"),
-    ("HC", 0, 4, "S"),
-    ("W", 0, 1, 1),
-    ("QH", 0, 0, 1),
-    ("XC", 3, "S"),
-    ("QH", 1, 0, 1),
-    ("HP", 0, 5, 2),
-    ("HC", 1, 4, "V"),
-    ("HP", 1, 5, 3),
-    ("WC", 0, 0, "S"),
-    ("W", 0, 2, 4),
-    ("QR", 0, 1, 1, "V"),
-    ("HC", 0, 5, "S"),
-    ("W", 0, 3, 5),
-    ("HC", 1, 5, "V"),
-    ("WC", 0, 1, "S"),
-    ("HP", 0, 6, 6),
-    ("QH", 0, 1, 0),
-    ("WC", 0, 2, "S"),
-    ("HP", 1, 6, 0),
-    ("QH", 1, 1, 0),
-    ("HP", 0, 7, 7),
-    ("QR", 1, 1, 0, "V"),
-    ("HC", 0, 6, "S"),
-    ("HP", 1, 7, 2),
-    ("W", 0, 4, 3),
-    ("HC", 1, 6, "V"),
-    ("HC", 0, 7, "S"),
-    ("W", 0, 5, 1),
-    ("HC", 1, 7, "V"),
-    ("WC", 0, 3, "S"),
-    ("XT", 4, 4),
-    ("QH", 0, 1, 1),
-    ("WC", 0, 4, "S"),
-    ("QH", 1, 1, 1),
-    ("XT", 5, 6),
-    ("QR", 1, 1, 1, "V"),
-    ("XT", 6, 0),
-    ("WC", 0, 5, "S"),
-    ("XT", 7, 7),
-    ("QQ", 0, 1),
-    ("W", 0, 6, 2),
-    ("QQ", 1, 1),
-    ("W", 0, 7, 5),
-    ("WC", 0, 6, "S"),
-    ("QX", 0),
-    ("W", 1, 0, 3),
-    ("WC", 0, 7, "S"),
-    ("QW", 0, 0),
-    ("W", 1, 1, 1),
-    ("WC", 1, 0, "S"),
-    ("QX", 1),
-    ("W", 1, 2, 2),
-    ("WC", 1, 1, "S"),
-    ("XC", 4, "V"),
-    ("W", 1, 3, 5),
-    ("XC", 5, "V"),
-    ("WC", 1, 2, "S"),
-    ("W", 1, 4, 3),
-    ("QX", 2),
-    ("WC", 1, 3, "S"),
-    ("W", 1, 5, 1),
-    ("XC", 6, "V"),
-    ("WC", 1, 4, "S"),
-    ("QW", 1, 0),
-    ("W", 1, 6, 4),
-    ("WC", 1, 5, "S"),
-    ("XC", 7, "V"),
-    ("W", 1, 7, 6),
-    ("WC", 1, 6, "S"),
-    ("QX", 3),
-    ("O", 0, 0, 2),
-    ("WC", 1, 7, "S"),
-    ("QW", 0, 1),
-    ("O", 1, 0, 5),
-    ("QW", 1, 1),
-    ("O", 2, 0, 0),
-    ("OC", 1, 0, "S"),
-    ("OC", 0, 0, "V"),
-    ("O", 3, 0, 3),
-    ("ST", 1, 0),
-    ("OC", 2, 0, "V"),
-    ("O", 4, 0, 1),
-    ("OC", 3, 0, "S"),
-    ("ST", 0, 0),
-    ("O", 5, 0, 7),
-    ("OC", 4, 0, "V"),
-    ("ST", 2, 0),
-    ("O", 6, 0, 4),
-    ("OC", 5, 0, "S"),
-    ("ST", 3, 0),
-    ("O", 7, 0, 6),
-    ("OC", 6, 0, "V"),
-    ("ST", 4, 0),
-    ("O", 0, 1, 5),
-    ("OC", 7, 0, "S"),
-    ("ST", 5, 0),
-    ("O", 1, 1, 2),
-    ("OC", 0, 1, "S"),
-    ("ST", 6, 0),
-    ("O", 2, 1, 0),
-    ("OC", 1, 1, "V"),
-    ("ST", 7, 0),
-    ("O", 3, 1, 3),
-    ("ST", 0, 1),
-    ("OC", 2, 1, "S"),
-    ("O", 4, 1, 1),
-    ("ST", 1, 1),
-    ("OC", 3, 1, "V"),
-    ("O", 5, 1, 7),
-    ("ST", 2, 1),
-    ("OC", 4, 1, "S"),
-    ("O", 6, 1, 4),
-    ("ST", 3, 1),
-    ("OC", 5, 1, "V"),
-    ("O", 7, 1, 6),
-    ("ST", 4, 1),
-    ("OC", 6, 1, "S"),
-    ("ST", 5, 1),
-    ("OC", 7, 1, "V"),
-    ("ST", 6, 1),
-    ("ST", 7, 1),
-]
+PACK = 4
+HALF = 512
+PASSES = N // HALF
+BLOCKS = N // P
 
 
 def tile_householderlinear_pa_kernel(tc, x, q_prev, v, out):
@@ -186,33 +29,29 @@ def tile_householderlinear_pa_kernel(tc, x, q_prev, v, out):
         ctx.enter_context(tc.manual_schedule())
         const = ctx.enter_context(tc.tile_pool(name="const", bufs=1))
         keep = ctx.enter_context(tc.tile_pool(name="keep", bufs=1))
-        psum = ctx.enter_context(tc.psum_pool(name="psum", bufs=1))
+        psum = ctx.enter_context(tc.psum_pool(name="psum", bufs=8))
 
-        vcol = const.tile([P, 8], BF16)
-        nc.sync.dma_start(out=vcol[:], in_=v.rearrange("(p m) -> p m", m=8))
-        vrow = const.tile([P, N], BF16)
-        nc.vector.memset(vrow[:].bitcast(I32), 0)
-        nc.sync.dma_start(out=vrow[0:1, :], in_=v.rearrange("(o n) -> o n", o=1))
-        warm_in = const.tile([P, 1], F32)
-        warm_out = const.tile([P, 1], F32)
-        nc.gpsimd.memset(warm_in[:], 0.0)
-        nc.scalar.activation(out=warm_out[:], in_=warm_in[:], func=COPY)
+        v_cols = const.tile([P, N // P], BF16)
+        nc.sync.dma_start(out=v_cols[:], in_=v.rearrange("(p m) -> p m", p=P))
+        v_row = const.tile([P, N], BF16)
+        nc.vector.memset(v_row[:].bitcast(I32), 0)
+        nc.sync.dma_start(out=v_row[0:1, :], in_=v.rearrange("(o n) -> o n", o=1))
 
-        raw_q = {}
-        for c in range(2):
-            for g in range(2):
-                raw_q[(c, g)] = keep.tile([P, 4, 512], BF16, name="raw_q%d%d" % (c, g))
-        q_view = q_prev.rearrange("(c t p) k -> c p t k", c=2, t=4, p=P)
-        x_sb = keep.tile([P, 8, N], BF16)
-        x_view = x.rearrange("(p b) k -> p b k", b=8)
-        out_view = out.rearrange("(p b) i -> p b i", b=8)
+        q_view = q_prev.rearrange("(c t p) k -> c p t k", c=PASSES, t=PACK, p=P)
+        q_raw = {}
+        for c in range(PASSES):
+            for g in range(PASSES):
+                q_raw[(c, g)] = keep.tile([P, PACK, HALF], BF16, name="q_raw%d%d" % (c, g))
+        x_view = x.rearrange("(p r) k -> p r k", r=BLOCKS)
+        out_view = out.rearrange("(p r) i -> p r i", r=BLOCKS)
+        x_raw = keep.tile([P, BLOCKS, N], BF16)
 
         def load_q(c, g):
-            cols = slice(512 * g, 512 * g + 512)
-            nc.sync.dma_start(out=raw_q[(c, g)][:], in_=q_view[c][:, :, cols])
+            nc.sync.dma_start(out=q_raw[(c, g)][:], in_=q_view[c][:, :, g * HALF : (g + 1) * HALF])
 
-        def load_x(j):
-            nc.sync.dma_start(out=x_sb[:, 2 * j : 2 * j + 2, :], in_=x_view[:, 2 * j : 2 * j + 2, :])
+        def load_x(pair):
+            rows = slice(2 * pair, 2 * pair + 2)
+            nc.sync.dma_start(out=x_raw[:, rows, :], in_=x_view[:, rows, :])
 
         load_q(0, 0)
         load_q(1, 0)
@@ -223,174 +62,218 @@ def tile_householderlinear_pa_kernel(tc, x, q_prev, v, out):
         load_x(2)
         load_x(3)
 
+        dummy_in = const.tile([P, 1], F32)
+        dummy_out = const.tile([P, 1], F32)
+        nc.gpsimd.memset(dummy_in[:], 0.0)
+        nc.scalar.activation(out=dummy_out[:], in_=dummy_in[:], func=COPY)
         ident = const.tile([P, P], F32)
         make_identity(nc, ident[:])
-        dmask = const.tile([P, 4, P, 4], BF16)
-        nc.vector.memset(dmask[:].rearrange("p r i t -> p (r i t)").bitcast(I32), 0)
-        for r in range(4):
-            nc.vector.tensor_copy(out=dmask[:, r, :, r], in_=ident[:])
-        half = const.tile([P, 1], F32)
-        c2 = const.tile([P, 1], F32)
+        diag = const.tile([P, PACK, P, PACK], BF16)
+        nc.vector.memset(diag[:].rearrange("p d i t -> p (d i t)").bitcast(I32), 0)
+        for d in range(PACK):
+            nc.vector.tensor_copy(out=diag[:, d, :, d], in_=ident[:])
+        minus_half_sum = const.tile([P, 1], F32)
+        scale = const.tile([P, 1], F32)
 
-        h_in = keep.tile([P, 2, N, 4], BF16, align_bytes=64)
-        h_codes = keep.tile([P, 2, N], U32, align_bytes=64)
-        h_scales = keep.tile([P, 2, N], U8, align_bytes=64)
-        q_in = keep.tile([P, 2, N, 4], BF16, align_bytes=64)
-        q_codes = keep.tile([P, 2, N], U32, align_bytes=64)
-        q_scales = keep.tile([P, 2, N], U8, align_bytes=64)
-        x_in = keep.tile([P, 8, N], BF16, align_bytes=64)
-        x_codes = keep.tile([P, 8, 2, P], U32, align_bytes=64)
-        x_scales = keep.tile([P, 8, 2, P], U8, align_bytes=64)
-        w_in = keep.tile([P, 2, N, 4], BF16, align_bytes=64)
-        w_codes = keep.tile([P, 2, N], U32, align_bytes=64)
-        w_scales = keep.tile([P, 2, N], U8, align_bytes=64)
-        o_all = keep.tile([P, 8, N], F32)
+        h_bf = keep.tile([P, PASSES, N, PACK], BF16, align_bytes=64)
+        h_words = keep.tile([P, PASSES, N], U32, align_bytes=64)
+        h_scales = keep.tile([P, PASSES, N], U8, align_bytes=64)
+        q_bf = keep.tile([P, PASSES, N, PACK], BF16, align_bytes=64)
+        q_words = keep.tile([P, PASSES, N], U32, align_bytes=64)
+        q_scales = keep.tile([P, PASSES, N], U8, align_bytes=64)
+        x_bf = keep.tile([P, BLOCKS, N], BF16, align_bytes=64)
+        x_words = keep.tile([P, BLOCKS, PASSES, P], U32, align_bytes=64)
+        x_scales = keep.tile([P, BLOCKS, PASSES, P], U8, align_bytes=64)
+        w_bf = keep.tile([P, PASSES, N, PACK], BF16, align_bytes=64)
+        w_words = keep.tile([P, PASSES, N], U32, align_bytes=64)
+        w_scales = keep.tile([P, PASSES, N], U8, align_bytes=64)
+        out_sb = keep.tile([P, BLOCKS, N], F32)
 
         banks = {}
 
-        def bank(key, k, shape):
-            t = psum.tile(shape, F32, tag="bank%d" % k, name="ps%s%d" % (key[0], len(banks)))
-            banks[key] = t
-            return t
+        def new_bank(key, shape):
+            banks[key] = psum.tile(shape, F32, tag="bank", name="bank_%s%d" % (key[0], len(banks)))
+            return banks[key]
 
-        def copy_on(eng, dst, src):
-            if eng == "V":
+        def copy_on(on_vector, dst, src):
+            if on_vector:
                 nc.vector.tensor_copy(out=dst, in_=src)
             else:
                 nc.scalar.copy(out=dst, in_=src)
 
-        def quantise(src, codes, scales):
-            nc.vector.quantize_mx(out=codes.bitcast(FP8X4), scales=scales, in_=src)
+        def quantise(src, words, scales):
+            nc.vector.quantize_mx(out=words.bitcast(FP8X4), scales=scales, in_=src)
 
-        for op in PROGRAM:
-            kind = op[0]
-            if kind == "S8":
-                s_ps = bank(("S",), op[1], [P, 1])
-                for m in range(8):
-                    nc.tensor.matmul(
-                        out=s_ps[:],
-                        lhsT=vcol[:, m : m + 1].to_broadcast([P, P]),
-                        rhs=vcol[:, m : m + 1],
-                        start=(m == 0),
-                        stop=(m == 7),
-                    )
-            elif kind == "C2":
-                nc.vector.tensor_scalar(out=half[:], in0=banks[("S",)][:], scalar1=-0.5, scalar2=None, op0=MULT)
-                nc.vector.reciprocal(out=c2[:], in_=half[:])
-            elif kind == "HP":
-                c, ib = op[1], op[2]
-                hb = bank(("H", c, ib), op[3], [P, 4, P])
-                for t in range(4):
-                    jb = 4 * c + t
-                    nc.tensor.matmul(
-                        out=hb[:, t, :],
-                        lhsT=vrow[:, jb * P : (jb + 1) * P],
-                        rhs=vrow[:, ib * P : (ib + 1) * P],
-                        start=True,
-                        stop=True,
-                    )
-            elif kind == "HC":
-                c, ib = op[1], op[2]
-                dst = h_in[:, c, ib * P : (ib + 1) * P, :]
-                src = banks[("H", c, ib)][:].rearrange("p t i -> p i t")
-                r = ib - 4 * c
-                if 0 <= r < 4:
-                    nc.vector.scalar_tensor_tensor(
-                        out=dst, in0=src, scalar=c2[:, 0:1], in1=dmask[:, r], op0=MULT, op1=ADD
-                    )
-                elif op[3] == "V":
-                    nc.vector.tensor_scalar(out=dst, in0=src, scalar1=c2[:, 0:1], scalar2=None, op0=MULT)
-                else:
-                    nc.scalar.activation(out=dst, in_=src, func=COPY, scale=c2[:, 0:1])
-            elif kind == "QH":
-                c = op[1]
-                cols = slice(512 * op[2] + 256 * op[3], 512 * op[2] + 256 * op[3] + 256)
-                quantise(
-                    h_in[:, c, cols, :].rearrange("p i t -> p (i t)"), h_codes[:, c, cols], h_scales[:, c, cols]
+        def sum_of_squares():
+            total = new_bank(("s",), [P, 1])
+            for m in range(N // P):
+                nc.tensor.matmul(
+                    out=total[:],
+                    lhsT=v_cols[:, m : m + 1].to_broadcast([P, P]),
+                    rhs=v_cols[:, m : m + 1],
+                    start=(m == 0),
+                    stop=(m == N // P - 1),
                 )
-            elif kind == "QR":
-                c, g, u = op[1], op[2], op[3]
-                cols = slice(512 * g + 256 * u, 512 * g + 256 * u + 256)
-                copy_on(
-                    op[4],
-                    q_in[:, c, cols, :].rearrange("p (e k) t -> p e k t", e=2),
-                    raw_q[(c, g)][:, :, 256 * u : 256 * u + 256].rearrange("p t (k e) -> p e k t", e=2),
-                )
-            elif kind == "QQ":
-                c = op[1]
-                cols = slice(512 * op[2], 512 * op[2] + 512)
-                quantise(
-                    q_in[:, c, cols, :].rearrange("p k t -> p (k t)"), q_codes[:, c, cols], q_scales[:, c, cols]
-                )
-            elif kind == "XT":
-                bt = op[1]
-                xt = bank(("X", bt), op[2], [P, 4, P])
-                words = x_sb[:, bt, :].bitcast(F32)
-                for gu in range(4):
-                    nc.tensor.transpose(xt[:, gu, :], words[:, gu * P : (gu + 1) * P], ident[:])
-            elif kind == "XC":
-                bt = op[1]
-                copy_on(
-                    op[2],
-                    x_in[:, bt, :].bitcast(F32).rearrange("p (g b u) -> p g b u", g=2, u=2),
-                    banks[("X", bt)][:].rearrange("p (g u) b -> p g b u", g=2),
-                )
-            elif kind == "QX":
-                j = op[1]
-                quantise(
-                    x_in[:, 2 * j : 2 * j + 2, :].rearrange("p b k -> p (b k)"),
-                    x_codes[:, 2 * j : 2 * j + 2].rearrange("p b g m -> p (b g m)"),
-                    x_scales[:, 2 * j : 2 * j + 2].rearrange("p b g m -> p (b g m)"),
-                )
-            elif kind == "W":
-                g, ib = op[1], op[2]
-                wb = bank(("W", g, ib), op[3], [P, 4, P])
-                icols = slice(ib * P, (ib + 1) * P)
-                for t in range(4):
-                    kcols = slice(512 * g + P * t, 512 * g + P * t + P)
-                    for c in range(2):
-                        nc.tensor.matmul_mx(
-                            out=wb[:, t, :],
-                            lhsT=q_codes[:, c, kcols].bitcast(FP8X4),
-                            lhsT_scale=q_scales[:, c, kcols],
-                            rhs=h_codes[:, c, icols].bitcast(FP8X4),
-                            rhs_scale=h_scales[:, c, icols],
-                            start=(c == 0),
-                            stop=(c == 1),
+
+        def reflection_scale():
+            nc.vector.tensor_scalar(
+                out=minus_half_sum[:], in0=banks[("s",)][:], scalar1=-0.5, scalar2=None, op0=MULT
+            )
+            nc.vector.reciprocal(out=scale[:], in_=minus_half_sum[:])
+
+        def passes_of(ib):
+            return (1, 0) if ib < PACK else (0, 1)
+
+        def h_products(pair):
+            for ib in (2 * pair, 2 * pair + 1):
+                for c in passes_of(ib):
+                    bank = new_bank(("h", c, ib), [P, PACK, P])
+                    for t in range(PACK):
+                        jb = PACK * c + t
+                        nc.tensor.matmul(
+                            out=bank[:, t, :],
+                            lhsT=v_row[:, jb * P : (jb + 1) * P],
+                            rhs=v_row[:, ib * P : (ib + 1) * P],
+                            start=True,
+                            stop=True,
                         )
-            elif kind == "WC":
-                g, ib = op[1], op[2]
-                copy_on(
-                    op[3],
-                    w_in[:, g, ib * P : (ib + 1) * P, :],
-                    banks[("W", g, ib)][:].rearrange("p t i -> p i t"),
-                )
-            elif kind == "QW":
-                g = op[1]
-                cols = slice(512 * op[2], 512 * op[2] + 512)
+
+        def h_copies(pair):
+            for ib in (2 * pair, 2 * pair + 1):
+                for c in passes_of(ib):
+                    dst = h_bf[:, c, ib * P : (ib + 1) * P, :]
+                    src = banks[("h", c, ib)][:].rearrange("p t i -> p i t")
+                    d = ib - PACK * c
+                    if 0 <= d < PACK:
+                        nc.vector.scalar_tensor_tensor(
+                            out=dst, in0=src, scalar=scale[:, 0:1], in1=diag[:, d], op0=MULT, op1=ADD
+                        )
+                    else:
+                        nc.scalar.activation(out=dst, in_=src, func=COPY, scale=scale[:, 0:1])
+
+        def quantise_h(pair):
+            cols = slice(2 * pair * P, (2 * pair + 2) * P)
+            for c in range(PASSES):
                 quantise(
-                    w_in[:, g, cols, :].rearrange("p i t -> p (i t)"), w_codes[:, g, cols], w_scales[:, g, cols]
+                    h_bf[:, c, cols, :].rearrange("p i t -> p (i t)"), h_words[:, c, cols], h_scales[:, c, cols]
                 )
-            elif kind == "O":
-                bt, ih = op[1], op[2]
-                ob = bank(("O", bt, ih), op[3], [P, 512])
-                cols = slice(512 * ih, 512 * ih + 512)
-                for g in range(2):
-                    nc.tensor.matmul_mx(
-                        out=ob[:],
-                        lhsT=x_codes[:, bt, g, :].bitcast(FP8X4),
-                        lhsT_scale=x_scales[:, bt, g, :],
-                        rhs=w_codes[:, g, cols].bitcast(FP8X4),
-                        rhs_scale=w_scales[:, g, cols],
-                        start=(g == 0),
-                        stop=(g == 1),
-                    )
-            elif kind == "OC":
-                bt, ih = op[1], op[2]
-                copy_on(op[3], o_all[:, bt, 512 * ih : 512 * ih + 512], banks[("O", bt, ih)][:])
-            elif kind == "ST":
-                bt, ih = op[1], op[2]
-                cols = slice(512 * ih, 512 * ih + 512)
-                nc.sync.dma_start(out=out_view[:, bt, cols], in_=o_all[:, bt, cols])
+
+        def regroup_q(c, g, u):
+            places = slice(g * HALF + 2 * u * P, g * HALF + (2 * u + 2) * P)
+            nc.vector.tensor_copy(
+                out=q_bf[:, c, places, :].rearrange("p (e k) t -> p e k t", e=2),
+                in_=q_raw[(c, g)][:, :, 2 * u * P : (2 * u + 2) * P].rearrange("p t (k e) -> p e k t", e=2),
+            )
+
+        def quantise_q(g):
+            places = slice(g * HALF, (g + 1) * HALF)
+            for c in range(PASSES):
+                quantise(
+                    q_bf[:, c, places, :].rearrange("p k t -> p (k t)"),
+                    q_words[:, c, places],
+                    q_scales[:, c, places],
+                )
+
+        def x_transposes(row_tiles):
+            for r in row_tiles:
+                bank = new_bank(("x", r), [P, PACK, P])
+                words = x_raw[:, r, :].bitcast(F32)
+                for gu in range(PACK):
+                    nc.tensor.transpose(bank[:, gu, :], words[:, gu * P : (gu + 1) * P], ident[:])
+
+        def x_copy(r, on_vector):
+            copy_on(
+                on_vector,
+                x_bf[:, r, :].bitcast(F32).rearrange("p (g b u) -> p g b u", g=PASSES, u=2),
+                banks[("x", r)][:].rearrange("p (g u) b -> p g b u", g=PASSES),
+            )
+
+        def quantise_x(pair):
+            rows = slice(2 * pair, 2 * pair + 2)
+            quantise(
+                x_bf[:, rows, :].rearrange("p r k -> p (r k)"),
+                x_words[:, rows].rearrange("p r g b -> p (r g b)"),
+                x_scales[:, rows].rearrange("p r g b -> p (r g b)"),
+            )
+
+        def w_blocks(g, pair):
+            for ib in (2 * pair, 2 * pair + 1):
+                bank = new_bank(("w", g, ib), [P, PACK, P])
+                cols = slice(ib * P, (ib + 1) * P)
+                for t in range(PACK):
+                    places = slice(g * HALF + t * P, g * HALF + (t + 1) * P)
+                    for c in range(PASSES):
+                        nc.tensor.matmul_mx(
+                            out=bank[:, t, :],
+                            lhsT=q_words[:, c, places].bitcast(FP8X4),
+                            lhsT_scale=q_scales[:, c, places],
+                            rhs=h_words[:, c, cols].bitcast(FP8X4),
+                            rhs_scale=h_scales[:, c, cols],
+                            start=(c == 0),
+                            stop=(c == PASSES - 1),
+                        )
+                nc.scalar.copy(out=w_bf[:, g, cols, :], in_=bank[:].rearrange("p t i -> p i t"))
+
+        def quantise_w(g, half):
+            cols = slice(half * HALF, (half + 1) * HALF)
+            quantise(
+                w_bf[:, g, cols, :].rearrange("p i t -> p (i t)"), w_words[:, g, cols], w_scales[:, g, cols]
+            )
+
+        def out_block(r, half):
+            bank = new_bank(("o", r, half), [P, HALF])
+            cols = slice(half * HALF, (half + 1) * HALF)
+            for g in range(PASSES):
+                nc.tensor.matmul_mx(
+                    out=bank[:],
+                    lhsT=x_words[:, r, g, :].bitcast(FP8X4),
+                    lhsT_scale=x_scales[:, r, g, :],
+                    rhs=w_words[:, g, cols].bitcast(FP8X4),
+                    rhs_scale=w_scales[:, g, cols],
+                    start=(g == 0),
+                    stop=(g == PASSES - 1),
+                )
+            copy_on(r % 2 == 0, out_sb[:, r, cols], bank[:])
+            nc.sync.dma_start(out=out_view[:, r, cols], in_=out_sb[:, r, cols])
+
+        sum_of_squares()
+        regroup_q(0, 0, 0)
+        regroup_q(0, 0, 1)
+        reflection_scale()
+        regroup_q(1, 0, 0)
+        regroup_q(1, 0, 1)
+        h_products(0)
+        x_transposes(range(0, 4))
+        quantise_q(0)
+        h_copies(0)
+        for r in range(0, 4):
+            x_copy(r, False)
+        for pair in range(4):
+            quantise_h(pair)
+            if pair < 3:
+                h_products(pair + 1)
+                h_copies(pair + 1)
             else:
-                assert False, kind
+                x_transposes(range(4, 8))
+                x_copy(4, False)
+                x_copy(5, False)
+            w_blocks(0, pair)
+            regroup_q(pair // 2, 1, pair % 2)
+        quantise_q(1)
+        x_copy(6, True)
+        x_copy(7, True)
+        quantise_x(0)
+        quantise_w(0, 0)
+        quantise_x(1)
+        quantise_w(0, 1)
+        w_blocks(1, 0)
+        w_blocks(1, 1)
+        quantise_x(2)
+        quantise_x(3)
+        quantise_w(1, 0)
+        w_blocks(1, 2)
+        w_blocks(1, 3)
+        quantise_w(1, 1)
+        for half in range(2):
+            for r in range(BLOCKS):
+                out_block(r, half)

@@ -268,12 +268,15 @@ def tile_householderlinear_pa_kernel(tc, x, q_prev, v, out):
         quantise_w(0, 1)
         w_blocks(1, 0)
         w_blocks(1, 1)
+        quantise_w(1, 0)
         quantise_x(2)
         quantise_x(3)
-        quantise_w(1, 0)
-        w_blocks(1, 2)
-        w_blocks(1, 3)
+        for pair in (2, 3):
+            w_blocks(1, pair)
+            out_block(2 * pair - 4, 0)
+            out_block(2 * pair - 3, 0)
         quantise_w(1, 1)
-        for half in range(2):
-            for r in range(BLOCKS):
-                out_block(r, half)
+        for r in range(4, BLOCKS):
+            out_block(r, 0)
+        for r in range(BLOCKS):
+            out_block(r, 1)

@@ -161,8 +161,8 @@ def tile_householderlinear_pa_kernel(tc, x, q_prev, v, out):
         def regroup_q(c, g, u):
             places = slice(g * HALF + 2 * u * P, g * HALF + (2 * u + 2) * P)
             nc.vector.tensor_copy(
-                out=q_bf[:, c, places, :].rearrange("p (e k) t -> p e k t", e=2),
-                in_=q_raw[(c, g)][:, :, 2 * u * P : (2 * u + 2) * P].rearrange("p t (k e) -> p e k t", e=2),
+                out=q_bf[:, c, places, :].rearrange("p (e n i) t -> p e n t i", e=2, i=4),
+                in_=q_raw[(c, g)][:, :, 2 * u * P : (2 * u + 2) * P].rearrange("p t (n i e) -> p e n t i", e=2, i=4),
             )
 
         def quantise_q(g):

@@ -18,9 +18,13 @@ COPY = mybir.ActivationFunctionType.Copy
 P = 128
 N = 1024
 PACK = 4
-HALF = 512
-PASSES = N // HALF
-BLOCKS = N // P
+K_PASS = P * PACK
+PASSES = N // K_PASS
+BANK = 512
+SIDES = N // BANK
+STRIPS = N // P
+ROW_TILES = N // P
+EARLY_ROW_TILES = 4
 
 
 def tile_householderlinear_pa_kernel(tc, x, q_prev, v, out):
@@ -40,27 +44,27 @@ def tile_householderlinear_pa_kernel(tc, x, q_prev, v, out):
         q_view = q_prev.rearrange("(c t p) k -> c p t k", c=PASSES, t=PACK, p=P)
         q_raw = {}
         for c in range(PASSES):
-            for g in range(PASSES):
-                q_raw[(c, g)] = keep.tile([P, PACK, HALF], BF16, name="q_raw%d%d" % (c, g))
-        x_view = x.rearrange("(p r) k -> p r k", r=BLOCKS)
-        out_view = out.rearrange("(p r) i -> p r i", r=BLOCKS)
-        x_raw = keep.tile([P, BLOCKS, N], BF16)
+            for g in range(SIDES):
+                q_raw[(c, g)] = keep.tile([P, PACK, BANK], BF16, name="q_raw%d%d" % (c, g))
+        x_view = x.rearrange("(p r) k -> p r k", r=ROW_TILES)
+        out_view = out.rearrange("(p r) i -> p r i", r=ROW_TILES)
+        x_raw = keep.tile([P, ROW_TILES, N], BF16)
 
         def load_q(c, g):
-            nc.sync.dma_start(out=q_raw[(c, g)][:], in_=q_view[c][:, :, g * HALF : (g + 1) * HALF])
+            nc.sync.dma_start(out=q_raw[(c, g)][:], in_=q_view[c][:, :, g * BANK : (g + 1) * BANK])
 
-        def load_x(pair):
-            rows = slice(2 * pair, 2 * pair + 2)
+        def load_x(first):
+            rows = slice(first, first + 2)
             nc.sync.dma_start(out=x_raw[:, rows, :], in_=x_view[:, rows, :])
 
         load_q(0, 0)
         load_q(1, 0)
         load_x(0)
-        load_x(1)
+        load_x(2)
         load_q(0, 1)
         load_q(1, 1)
-        load_x(2)
-        load_x(3)
+        load_x(4)
+        load_x(6)
 
         dummy_in = const.tile([P, 1], F32)
         dummy_out = const.tile([P, 1], F32)
@@ -73,7 +77,7 @@ def tile_householderlinear_pa_kernel(tc, x, q_prev, v, out):
         for d in range(PACK):
             nc.vector.tensor_copy(out=diag[:, d, :, d], in_=ident[:])
         minus_half_sum = const.tile([P, 1], F32)
-        scale = const.tile([P, 1], F32)
+        coeff = const.tile([P, 1], F32)
 
         h_bf = keep.tile([P, PASSES, N, PACK], BF16, align_bytes=64)
         h_words = keep.tile([P, PASSES, N], U32, align_bytes=64)
@@ -81,13 +85,13 @@ def tile_householderlinear_pa_kernel(tc, x, q_prev, v, out):
         q_bf = keep.tile([P, PASSES, N, PACK], BF16, align_bytes=64)
         q_words = keep.tile([P, PASSES, N], U32, align_bytes=64)
         q_scales = keep.tile([P, PASSES, N], U8, align_bytes=64)
-        x_bf = keep.tile([P, BLOCKS, N], BF16, align_bytes=64)
-        x_words = keep.tile([P, BLOCKS, PASSES, P], U32, align_bytes=64)
-        x_scales = keep.tile([P, BLOCKS, PASSES, P], U8, align_bytes=64)
+        x_bf = keep.tile([P, ROW_TILES, N], BF16, align_bytes=64)
+        x_words = keep.tile([P, ROW_TILES, PASSES, P], U32, align_bytes=64)
+        x_scales = keep.tile([P, ROW_TILES, PASSES, P], U8, align_bytes=64)
         w_bf = keep.tile([P, PASSES, N, PACK], BF16, align_bytes=64)
         w_words = keep.tile([P, PASSES, N], U32, align_bytes=64)
         w_scales = keep.tile([P, PASSES, N], U8, align_bytes=64)
-        out_sb = keep.tile([P, BLOCKS, N], F32)
+        out_sb = keep.tile([P, ROW_TILES, N], F32)
 
         banks = {}
 
@@ -115,58 +119,59 @@ def tile_householderlinear_pa_kernel(tc, x, q_prev, v, out):
                     stop=(m == N // P - 1),
                 )
 
-        def reflection_scale():
+        def reflection_coeff():
             nc.vector.tensor_scalar(
                 out=minus_half_sum[:], in0=banks[("s",)][:], scalar1=-0.5, scalar2=None, op0=MULT
             )
-            nc.vector.reciprocal(out=scale[:], in_=minus_half_sum[:])
+            nc.vector.reciprocal(out=coeff[:], in_=minus_half_sum[:])
 
-        def passes_of(ib):
-            return (1, 0) if ib < PACK else (0, 1)
+        def passes_of(strip):
+            return (1, 0) if strip < PACK else (0, 1)
 
-        def h_products(pair):
-            for ib in (2 * pair, 2 * pair + 1):
-                for c in passes_of(ib):
-                    bank = new_bank(("h", c, ib), [P, PACK, P])
+        def h_products(strip_pair):
+            for strip in (2 * strip_pair, 2 * strip_pair + 1):
+                for c in passes_of(strip):
+                    bank = new_bank(("h", c, strip), [P, PACK, P])
                     for t in range(PACK):
-                        jb = PACK * c + t
+                        j_strip = PACK * c + t
                         nc.tensor.matmul(
                             out=bank[:, t, :],
-                            lhsT=v_row[:, jb * P : (jb + 1) * P],
-                            rhs=v_row[:, ib * P : (ib + 1) * P],
+                            lhsT=v_row[:, j_strip * P : (j_strip + 1) * P],
+                            rhs=v_row[:, strip * P : (strip + 1) * P],
                             start=True,
                             stop=True,
                         )
 
-        def h_copies(pair):
-            for ib in (2 * pair, 2 * pair + 1):
-                for c in passes_of(ib):
-                    dst = h_bf[:, c, ib * P : (ib + 1) * P, :]
-                    src = banks[("h", c, ib)][:].rearrange("p t i -> p i t")
-                    d = ib - PACK * c
+        def h_copies(strip_pair):
+            for strip in (2 * strip_pair, 2 * strip_pair + 1):
+                for c in passes_of(strip):
+                    dst = h_bf[:, c, strip * P : (strip + 1) * P, :]
+                    src = banks[("h", c, strip)][:].rearrange("p t i -> p i t")
+                    d = strip - PACK * c
                     if 0 <= d < PACK:
                         nc.vector.scalar_tensor_tensor(
-                            out=dst, in0=src, scalar=scale[:, 0:1], in1=diag[:, d], op0=MULT, op1=ADD
+                            out=dst, in0=src, scalar=coeff[:, 0:1], in1=diag[:, d], op0=MULT, op1=ADD
                         )
                     else:
-                        nc.scalar.activation(out=dst, in_=src, func=COPY, scale=scale[:, 0:1])
+                        nc.scalar.activation(out=dst, in_=src, func=COPY, scale=coeff[:, 0:1])
 
-        def quantise_h(pair):
-            cols = slice(2 * pair * P, (2 * pair + 2) * P)
+        def quantise_h(strip_pair):
+            cols = slice(2 * strip_pair * P, (2 * strip_pair + 2) * P)
             for c in range(PASSES):
                 quantise(
                     h_bf[:, c, cols, :].rearrange("p i t -> p (i t)"), h_words[:, c, cols], h_scales[:, c, cols]
                 )
 
         def regroup_q(c, g, u):
-            places = slice(g * HALF + 2 * u * P, g * HALF + (2 * u + 2) * P)
+            cols = slice(2 * u * P, (2 * u + 2) * P)
+            places = slice(g * K_PASS + 2 * u * P, g * K_PASS + (2 * u + 2) * P)
             nc.vector.tensor_copy(
                 out=q_bf[:, c, places, :].rearrange("p (e n i) t -> p e n t i", e=2, i=4),
-                in_=q_raw[(c, g)][:, :, 2 * u * P : (2 * u + 2) * P].rearrange("p t (n i e) -> p e n t i", e=2, i=4),
+                in_=q_raw[(c, g)][:, :, cols].rearrange("p t (n i e) -> p e n t i", e=2, i=4),
             )
 
         def quantise_q(g):
-            places = slice(g * HALF, (g + 1) * HALF)
+            places = slice(g * K_PASS, (g + 1) * K_PASS)
             for c in range(PASSES):
                 quantise(
                     q_bf[:, c, places, :].rearrange("p k t -> p (k t)"),
@@ -188,20 +193,20 @@ def tile_householderlinear_pa_kernel(tc, x, q_prev, v, out):
                 banks[("x", r)][:].rearrange("p (g u) b -> p g b u", g=PASSES),
             )
 
-        def quantise_x(pair):
-            rows = slice(2 * pair, 2 * pair + 2)
+        def quantise_x(first):
+            rows = slice(first, first + 2)
             quantise(
                 x_bf[:, rows, :].rearrange("p r k -> p (r k)"),
                 x_words[:, rows].rearrange("p r g b -> p (r g b)"),
                 x_scales[:, rows].rearrange("p r g b -> p (r g b)"),
             )
 
-        def w_blocks(g, pair):
-            for ib in (2 * pair, 2 * pair + 1):
-                bank = new_bank(("w", g, ib), [P, PACK, P])
-                cols = slice(ib * P, (ib + 1) * P)
+        def w_strips(g, strip_pair):
+            for strip in (2 * strip_pair, 2 * strip_pair + 1):
+                bank = new_bank(("w", g, strip), [P, PACK, P])
+                cols = slice(strip * P, (strip + 1) * P)
                 for t in range(PACK):
-                    places = slice(g * HALF + t * P, g * HALF + (t + 1) * P)
+                    places = slice(g * K_PASS + t * P, g * K_PASS + (t + 1) * P)
                     for c in range(PASSES):
                         nc.tensor.matmul_mx(
                             out=bank[:, t, :],
@@ -214,15 +219,15 @@ def tile_householderlinear_pa_kernel(tc, x, q_prev, v, out):
                         )
                 nc.scalar.copy(out=w_bf[:, g, cols, :], in_=bank[:].rearrange("p t i -> p i t"))
 
-        def quantise_w(g, half):
-            cols = slice(half * HALF, (half + 1) * HALF)
+        def quantise_w(g, side):
+            cols = slice(side * BANK, (side + 1) * BANK)
             quantise(
                 w_bf[:, g, cols, :].rearrange("p i t -> p (i t)"), w_words[:, g, cols], w_scales[:, g, cols]
             )
 
-        def out_block(r, half):
-            bank = new_bank(("o", r, half), [P, HALF])
-            cols = slice(half * HALF, (half + 1) * HALF)
+        def out_bank(r, side):
+            bank = new_bank(("o", r, side), [P, BANK])
+            cols = slice(side * BANK, (side + 1) * BANK)
             for g in range(PASSES):
                 nc.tensor.matmul_mx(
                     out=bank[:],
@@ -239,44 +244,49 @@ def tile_householderlinear_pa_kernel(tc, x, q_prev, v, out):
         sum_of_squares()
         regroup_q(0, 0, 0)
         regroup_q(0, 0, 1)
-        reflection_scale()
+        reflection_coeff()
         regroup_q(1, 0, 0)
         regroup_q(1, 0, 1)
         h_products(0)
-        x_transposes(range(0, 4))
+        x_transposes(range(EARLY_ROW_TILES))
         quantise_q(0)
         h_copies(0)
-        for r in range(0, 4):
+        for r in range(EARLY_ROW_TILES):
             x_copy(r, False)
-        for pair in range(4):
-            quantise_h(pair)
-            if pair < 3:
-                h_products(pair + 1)
-                h_copies(pair + 1)
+
+        last_pair = STRIPS // 2 - 1
+        for strip_pair in range(last_pair + 1):
+            quantise_h(strip_pair)
+            if strip_pair < last_pair:
+                h_products(strip_pair + 1)
+                h_copies(strip_pair + 1)
             else:
-                x_transposes(range(4, 8))
-                x_copy(4, False)
-                x_copy(5, False)
-            w_blocks(0, pair)
-            regroup_q(pair // 2, 1, pair % 2)
+                x_transposes(range(EARLY_ROW_TILES, ROW_TILES))
+                x_copy(EARLY_ROW_TILES, False)
+                x_copy(EARLY_ROW_TILES + 1, False)
+            w_strips(0, strip_pair)
+            regroup_q(strip_pair // 2, 1, strip_pair % 2)
+
         quantise_q(1)
-        x_copy(6, True)
-        x_copy(7, True)
+        x_copy(ROW_TILES - 2, True)
+        x_copy(ROW_TILES - 1, True)
         quantise_x(0)
         quantise_w(0, 0)
-        quantise_x(1)
-        quantise_w(0, 1)
-        w_blocks(1, 0)
-        w_blocks(1, 1)
-        quantise_w(1, 0)
         quantise_x(2)
-        quantise_x(3)
-        for pair in (2, 3):
-            w_blocks(1, pair)
-            out_block(2 * pair - 4, 0)
-            out_block(2 * pair - 3, 0)
+        quantise_w(0, 1)
+        w_strips(1, 0)
+        w_strips(1, 1)
+        quantise_w(1, 0)
+        quantise_x(4)
+        quantise_x(6)
+        for strip_pair in (last_pair - 1, last_pair):
+            w_strips(1, strip_pair)
+            first = 2 * (strip_pair - last_pair + 1)
+            out_bank(first, 0)
+            out_bank(first + 1, 0)
         quantise_w(1, 1)
-        for r in range(4, BLOCKS):
-            out_block(r, 0)
-        for r in range(BLOCKS):
-            out_block(r, 1)
+
+        for r in range(4, ROW_TILES):
+            out_bank(r, 0)
+        for r in range(ROW_TILES):
+            out_bank(r, 1)

@@ -37,9 +37,10 @@ def tile_householderlinear_pa_kernel(tc, x, q_prev, v, out):
 
         v_cols = const.tile([P, N // P], BF16)
         nc.sync.dma_start(out=v_cols[:], in_=v.rearrange("(p m) -> p m", p=P))
+        v_one = const.tile([1, N], BF16)
+        nc.sync.dma_start(out=v_one[:], in_=v.rearrange("(o n) -> o n", o=1))
         v_row = const.tile([P, N], BF16)
         nc.vector.memset(v_row[:].bitcast(I32), 0)
-        nc.sync.dma_start(out=v_row[0:1, :], in_=v.rearrange("(o n) -> o n", o=1))
 
         q_view = q_prev.rearrange("(c t p) k -> c p t k", c=PASSES, t=PACK, p=P)
         q_raw = {}
@@ -242,9 +243,10 @@ def tile_householderlinear_pa_kernel(tc, x, q_prev, v, out):
             nc.sync.dma_start(out=out_view[:, r, cols], in_=out_sb[:, r, cols])
 
         sum_of_squares()
+        nc.vector.tensor_copy(out=v_row[0:1, :], in_=v_one[:])
+        reflection_coeff()
         regroup_q(0, 0, 0)
         regroup_q(0, 0, 1)
-        reflection_coeff()
         regroup_q(1, 0, 0)
         regroup_q(1, 0, 1)
         h_products(0)

@@ -24,6 +24,7 @@ BANK = 512
 SIDES = N // BANK
 STRIPS = N // P
 ROW_TILES = N // P
+WARM_UPS = 2
 EARLY_ROW_TILES = 4
 
 
@@ -69,14 +70,20 @@ def tile_householderlinear_pa_kernel(tc, x, q_prev, v, out):
 
         dummy_in = const.tile([P, 1], F32)
         dummy_out = const.tile([P, 1], F32)
+        zeros = const.tile([P, BANK], BF16)
+        nc.gpsimd.memset(zeros[:].bitcast(I32), 0)
         nc.gpsimd.memset(dummy_in[:], 0.0)
         nc.scalar.activation(out=dummy_out[:], in_=dummy_in[:], func=COPY)
         ident = const.tile([P, P], F32)
         make_identity(nc, ident[:])
-        diag = const.tile([P, PACK, P, PACK], BF16)
-        nc.vector.memset(diag[:].rearrange("p d i t -> p (d i t)").bitcast(I32), 0)
-        for d in range(PACK):
-            nc.vector.tensor_copy(out=diag[:, d, :, d], in_=ident[:])
+        diag = const.tile([P, (P + 1) * PACK], BF16)
+        nc.vector.memset(diag[:].bitcast(I32), 0)
+
+        def diag_view(d):
+            first = PACK - 1 - d
+            return diag[:, first : first + P * PACK].rearrange("p (i t) -> p i t", t=PACK)
+
+        nc.vector.tensor_copy(out=diag_view(0)[:, :, 0], in_=ident[:])
         minus_half_sum = const.tile([P, 1], F32)
         coeff = const.tile([P, 1], F32)
 
@@ -109,6 +116,11 @@ def tile_householderlinear_pa_kernel(tc, x, q_prev, v, out):
         def quantise(src, words, scales):
             nc.vector.quantize_mx(out=words.bitcast(FP8X4), scales=scales, in_=src)
 
+        def warm_up():
+            bank = new_bank(("z",), [P, BANK])
+            for m in range(WARM_UPS):
+                nc.tensor.matmul(out=bank[:], lhsT=zeros[:, :P], rhs=zeros[:], start=True, stop=True)
+
         def sum_of_squares():
             total = new_bank(("s",), [P, 1])
             for m in range(N // P):
@@ -129,8 +141,8 @@ def tile_householderlinear_pa_kernel(tc, x, q_prev, v, out):
         def passes_of(strip):
             return (1, 0) if strip < PACK else (0, 1)
 
-        def h_products(strip_pair):
-            for strip in (2 * strip_pair, 2 * strip_pair + 1):
+        def h_products(strips):
+            for strip in strips:
                 for c in passes_of(strip):
                     bank = new_bank(("h", c, strip), [P, PACK, P])
                     for t in range(PACK):
@@ -143,15 +155,15 @@ def tile_householderlinear_pa_kernel(tc, x, q_prev, v, out):
                             stop=True,
                         )
 
-        def h_copies(strip_pair):
-            for strip in (2 * strip_pair, 2 * strip_pair + 1):
+        def h_copies(strips):
+            for strip in strips:
                 for c in passes_of(strip):
                     dst = h_bf[:, c, strip * P : (strip + 1) * P, :]
                     src = banks[("h", c, strip)][:].rearrange("p t i -> p i t")
                     d = strip - PACK * c
                     if 0 <= d < PACK:
                         nc.vector.scalar_tensor_tensor(
-                            out=dst, in0=src, scalar=coeff[:, 0:1], in1=diag[:, d], op0=MULT, op1=ADD
+                            out=dst, in0=src, scalar=coeff[:, 0:1], in1=diag_view(d), op0=MULT, op1=ADD
                         )
                     else:
                         nc.scalar.activation(out=dst, in_=src, func=COPY, scale=coeff[:, 0:1])
@@ -242,27 +254,35 @@ def tile_householderlinear_pa_kernel(tc, x, q_prev, v, out):
             copy_on(r % 2 == 0, out_sb[:, r, cols], bank[:])
             nc.sync.dma_start(out=out_view[:, r, cols], in_=out_sb[:, r, cols])
 
+        warm_up()
         sum_of_squares()
         nc.vector.tensor_copy(out=v_row[0:1, :], in_=v_one[:])
         reflection_coeff()
+        h_products(range(2))
         regroup_q(0, 0, 0)
         regroup_q(0, 0, 1)
+        h_copies(range(2))
         regroup_q(1, 0, 0)
         regroup_q(1, 0, 1)
-        h_products(0)
-        x_transposes(range(EARLY_ROW_TILES))
+        for strip in (2, 3):
+            row_tiles = range(2 * strip - 4, 2 * strip - 2)
+            x_transposes(row_tiles)
+            h_products((strip,))
+            for r in row_tiles:
+                x_copy(r, False)
+        quantise_h(0)
         quantise_q(0)
-        h_copies(0)
-        for r in range(EARLY_ROW_TILES):
-            x_copy(r, False)
+        h_copies((2, 3))
 
         last_pair = STRIPS // 2 - 1
         for strip_pair in range(last_pair + 1):
-            quantise_h(strip_pair)
-            if strip_pair < last_pair:
-                h_products(strip_pair + 1)
-                h_copies(strip_pair + 1)
-            else:
+            if strip_pair > 0:
+                quantise_h(strip_pair)
+            next_strips = (2 * strip_pair + 2, 2 * strip_pair + 3)
+            if 0 < strip_pair < last_pair:
+                h_products(next_strips)
+                h_copies(next_strips)
+            if strip_pair == last_pair:
                 x_transposes(range(EARLY_ROW_TILES, ROW_TILES))
                 x_copy(EARLY_ROW_TILES, False)
                 x_copy(EARLY_ROW_TILES + 1, False)
@@ -274,21 +294,23 @@ def tile_householderlinear_pa_kernel(tc, x, q_prev, v, out):
         x_copy(ROW_TILES - 1, True)
         quantise_x(0)
         quantise_w(0, 0)
-        quantise_x(2)
-        quantise_w(0, 1)
         w_strips(1, 0)
         w_strips(1, 1)
         quantise_w(1, 0)
+        quantise_x(2)
         quantise_x(4)
+        w_strips(1, last_pair - 1)
+        out_bank(0, 0)
+        out_bank(1, 0)
         quantise_x(6)
-        for strip_pair in (last_pair - 1, last_pair):
-            w_strips(1, strip_pair)
-            first = 2 * (strip_pair - last_pair + 1)
-            out_bank(first, 0)
-            out_bank(first + 1, 0)
+        quantise_w(0, 1)
+        w_strips(1, last_pair)
+        out_bank(2, 0)
+        out_bank(3, 0)
+        out_bank(4, 0)
         quantise_w(1, 1)
 
-        for r in range(4, ROW_TILES):
+        for r in range(5, ROW_TILES):
             out_bank(r, 0)
         for r in range(ROW_TILES):
             out_bank(r, 1)

@@ -294,23 +294,21 @@ def tile_householderlinear_pa_kernel(tc, x, q_prev, v, out):
         x_copy(ROW_TILES - 1, True)
         quantise_x(0)
         quantise_w(0, 0)
+        quantise_x(2)
+        quantise_w(0, 1)
         w_strips(1, 0)
         w_strips(1, 1)
         quantise_w(1, 0)
-        quantise_x(2)
         quantise_x(4)
-        w_strips(1, last_pair - 1)
-        out_bank(0, 0)
-        out_bank(1, 0)
         quantise_x(6)
-        quantise_w(0, 1)
-        w_strips(1, last_pair)
-        out_bank(2, 0)
-        out_bank(3, 0)
-        out_bank(4, 0)
+        for strip_pair in (last_pair - 1, last_pair):
+            w_strips(1, strip_pair)
+            first = 2 * (strip_pair - last_pair + 1)
+            out_bank(first, 0)
+            out_bank(first + 1, 0)
         quantise_w(1, 1)
 
-        for r in range(5, ROW_TILES):
+        for r in range(4, ROW_TILES):
             out_bank(r, 0)
         for r in range(ROW_TILES):
             out_bank(r, 1)

@@ -24,7 +24,8 @@ BANK = 512
 SIDES = N // BANK
 STRIPS = N // P
 ROW_TILES = N // P
-WARM_UPS = 2
+WARM_UPS = 3
+PLAIN_STRIPS = (0, 1)
 EARLY_ROW_TILES = 4
 
 
@@ -85,6 +86,7 @@ def tile_householderlinear_pa_kernel(tc, x, q_prev, v, out):
 
         nc.vector.tensor_copy(out=diag_view(0)[:, :, 0], in_=ident[:])
         minus_half_sum = const.tile([P, 1], F32)
+        minus_half_diag = const.tile([P, P], F32)
         coeff = const.tile([P, 1], F32)
 
         h_bf = keep.tile([P, PASSES, N, PACK], BF16, align_bytes=64)
@@ -137,6 +139,9 @@ def tile_householderlinear_pa_kernel(tc, x, q_prev, v, out):
                 out=minus_half_sum[:], in0=banks[("s",)][:], scalar1=-0.5, scalar2=None, op0=MULT
             )
             nc.vector.reciprocal(out=coeff[:], in_=minus_half_sum[:])
+            nc.scalar.activation(
+                out=minus_half_diag[:], in_=ident[:], func=COPY, scale=minus_half_sum[:, 0:1]
+            )
 
         def passes_of(strip):
             return (1, 0) if strip < PACK else (0, 1)
@@ -147,13 +152,18 @@ def tile_householderlinear_pa_kernel(tc, x, q_prev, v, out):
                     bank = new_bank(("h", c, strip), [P, PACK, P])
                     for t in range(PACK):
                         j_strip = PACK * c + t
+                        add_identity = j_strip == strip and strip in PLAIN_STRIPS
                         nc.tensor.matmul(
                             out=bank[:, t, :],
                             lhsT=v_row[:, j_strip * P : (j_strip + 1) * P],
                             rhs=v_row[:, strip * P : (strip + 1) * P],
                             start=True,
-                            stop=True,
+                            stop=not add_identity,
                         )
+                        if add_identity:
+                            nc.tensor.matmul(
+                                out=bank[:, t, :], lhsT=ident[:], rhs=minus_half_diag[:], start=False, stop=True
+                            )
 
         def h_copies(strips):
             for strip in strips:
@@ -161,7 +171,7 @@ def tile_householderlinear_pa_kernel(tc, x, q_prev, v, out):
                     dst = h_bf[:, c, strip * P : (strip + 1) * P, :]
                     src = banks[("h", c, strip)][:].rearrange("p t i -> p i t")
                     d = strip - PACK * c
-                    if 0 <= d < PACK:
+                    if 0 <= d < PACK and strip not in PLAIN_STRIPS:
                         nc.vector.scalar_tensor_tensor(
                             out=dst, in0=src, scalar=coeff[:, 0:1], in1=diag_view(d), op0=MULT, op1=ADD
                         )
@@ -270,8 +280,8 @@ def tile_householderlinear_pa_kernel(tc, x, q_prev, v, out):
             h_products((strip,))
             for r in row_tiles:
                 x_copy(r, False)
-        quantise_h(0)
         quantise_q(0)
+        quantise_h(0)
         h_copies((2, 3))
 
         last_pair = STRIPS // 2 - 1
@@ -295,17 +305,18 @@ def tile_householderlinear_pa_kernel(tc, x, q_prev, v, out):
         quantise_x(0)
         quantise_w(0, 0)
         quantise_x(2)
-        quantise_w(0, 1)
         w_strips(1, 0)
         w_strips(1, 1)
         quantise_w(1, 0)
+        quantise_w(0, 1)
         quantise_x(4)
+        w_strips(1, last_pair - 1)
+        out_bank(0, 0)
+        out_bank(1, 0)
         quantise_x(6)
-        for strip_pair in (last_pair - 1, last_pair):
-            w_strips(1, strip_pair)
-            first = 2 * (strip_pair - last_pair + 1)
-            out_bank(first, 0)
-            out_bank(first + 1, 0)
+        w_strips(1, last_pair)
+        out_bank(2, 0)
+        out_bank(3, 0)
         quantise_w(1, 1)
 
         for r in range(4, ROW_TILES):

@@ -26,7 +26,6 @@ STRIPS = N // P
 ROW_TILES = N // P
 WARM_UPS = 3
 PLAIN_STRIPS = (0, 1)
-EARLY_ROW_TILES = 4
 
 
 def tile_householderlinear_pa_kernel(tc, x, q_prev, v, out):
@@ -62,12 +61,10 @@ def tile_householderlinear_pa_kernel(tc, x, q_prev, v, out):
 
         load_q(0, 0)
         load_q(1, 0)
-        load_x(0)
-        load_x(2)
+        for first in range(0, ROW_TILES, 2):
+            load_x(first)
         load_q(0, 1)
         load_q(1, 1)
-        load_x(4)
-        load_x(6)
 
         dummy_in = const.tile([P, 1], F32)
         dummy_out = const.tile([P, 1], F32)
@@ -185,12 +182,13 @@ def tile_householderlinear_pa_kernel(tc, x, q_prev, v, out):
                     h_bf[:, c, cols, :].rearrange("p i t -> p (i t)"), h_words[:, c, cols], h_scales[:, c, cols]
                 )
 
-        def regroup_q(c, g, u):
+        def regroup_q(c, g, u, on_vector=True):
             cols = slice(2 * u * P, (2 * u + 2) * P)
             places = slice(g * K_PASS + 2 * u * P, g * K_PASS + (2 * u + 2) * P)
-            nc.vector.tensor_copy(
-                out=q_bf[:, c, places, :].rearrange("p (e n i) t -> p e n t i", e=2, i=4),
-                in_=q_raw[(c, g)][:, :, cols].rearrange("p t (n i e) -> p e n t i", e=2, i=4),
+            copy_on(
+                on_vector,
+                q_bf[:, c, places, :].rearrange("p (e n i) t -> p e n t i", e=2, i=4),
+                q_raw[(c, g)][:, :, cols].rearrange("p t (n i e) -> p e n t i", e=2, i=4),
             )
 
         def quantise_q(g):
@@ -224,8 +222,8 @@ def tile_householderlinear_pa_kernel(tc, x, q_prev, v, out):
                 x_scales[:, rows].rearrange("p r g b -> p (r g b)"),
             )
 
-        def w_strips(g, strip_pair):
-            for strip in (2 * strip_pair, 2 * strip_pair + 1):
+        def w_products(g, strips):
+            for strip in strips:
                 bank = new_bank(("w", g, strip), [P, PACK, P])
                 cols = slice(strip * P, (strip + 1) * P)
                 for t in range(PACK):
@@ -240,7 +238,11 @@ def tile_householderlinear_pa_kernel(tc, x, q_prev, v, out):
                             start=(c == 0),
                             stop=(c == PASSES - 1),
                         )
-                nc.scalar.copy(out=w_bf[:, g, cols, :], in_=bank[:].rearrange("p t i -> p i t"))
+
+        def w_copies(g, strips, on_vector):
+            for strip in strips:
+                cols = slice(strip * P, (strip + 1) * P)
+                copy_on(on_vector, w_bf[:, g, cols, :], banks[("w", g, strip)][:].rearrange("p t i -> p i t"))
 
         def quantise_w(g, side):
             cols = slice(side * BANK, (side + 1) * BANK)
@@ -268,58 +270,59 @@ def tile_householderlinear_pa_kernel(tc, x, q_prev, v, out):
         sum_of_squares()
         nc.vector.tensor_copy(out=v_row[0:1, :], in_=v_one[:])
         reflection_coeff()
-        h_products(range(2))
-        regroup_q(0, 0, 0)
-        regroup_q(0, 0, 1)
-        h_copies(range(2))
-        regroup_q(1, 0, 0)
-        regroup_q(1, 0, 1)
-        for strip in (2, 3):
-            row_tiles = range(2 * strip - 4, 2 * strip - 2)
+        h_products((0, 1))
+        h_copies((0, 1))
+        for c in range(PASSES):
+            for u in range(2):
+                regroup_q(c, 0, u)
+        for strips in ((2, 3), (4, 5)):
+            h_products(strips)
+            h_copies(strips)
+
+        def turn_x(row_tiles):
             x_transposes(row_tiles)
-            h_products((strip,))
             for r in row_tiles:
                 x_copy(r, False)
-        quantise_q(0)
+
+        turn_x((0, 1))
         quantise_h(0)
-        h_copies((2, 3))
+        h_products((6,))
+        h_copies((6,))
+        turn_x((2, 3, 4, 5))
+        h_products((7,))
+        quantise_q(0)
+        h_copies((7,))
+        turn_x((6, 7))
+        regroup_q(1, 1, 1, on_vector=False)
 
-        last_pair = STRIPS // 2 - 1
-        for strip_pair in range(last_pair + 1):
-            if strip_pair > 0:
-                quantise_h(strip_pair)
-            next_strips = (2 * strip_pair + 2, 2 * strip_pair + 3)
-            if 0 < strip_pair < last_pair:
-                h_products(next_strips)
-                h_copies(next_strips)
-            if strip_pair == last_pair:
-                x_transposes(range(EARLY_ROW_TILES, ROW_TILES))
-                x_copy(EARLY_ROW_TILES, False)
-                x_copy(EARLY_ROW_TILES + 1, False)
-            w_strips(0, strip_pair)
+        for strip_pair in range(3):
+            strips = (2 * strip_pair, 2 * strip_pair + 1)
+            w_products(0, strips)
+            w_copies(0, strips, False)
+            quantise_h(strip_pair + 1)
             regroup_q(strip_pair // 2, 1, strip_pair % 2)
-
         quantise_q(1)
-        x_copy(ROW_TILES - 2, True)
-        x_copy(ROW_TILES - 1, True)
+        w_products(0, (6, 7))
+
+        w_copies(0, (6,), True)
         quantise_x(0)
+        w_copies(0, (7,), True)
         quantise_w(0, 0)
         quantise_x(2)
-        w_strips(1, 0)
-        w_strips(1, 1)
+        w_products(1, (0, 1, 2, 3))
+        w_copies(1, (0, 1, 2), False)
+        w_copies(1, (3,), True)
         quantise_w(1, 0)
         quantise_w(0, 1)
-        quantise_x(4)
-        w_strips(1, last_pair - 1)
-        out_bank(0, 0)
-        out_bank(1, 0)
-        quantise_x(6)
-        w_strips(1, last_pair)
-        out_bank(2, 0)
-        out_bank(3, 0)
-        quantise_w(1, 1)
+        w_products(1, (4, 5, 6, 7))
+        w_copies(1, (4, 5, 6, 7), False)
 
-        for r in range(4, ROW_TILES):
-            out_bank(r, 0)
-        for r in range(ROW_TILES):
-            out_bank(r, 1)
+        for side in range(SIDES):
+            for r in range(ROW_TILES):
+                out_bank(r, side)
+                if (r, side) == (0, 0):
+                    quantise_x(4)
+                if (r, side) == (2, 0):
+                    quantise_x(6)
+                if (r, side) == (4, 0):
+                    quantise_w(1, 1)

@@ -223,21 +223,24 @@ def tile_householderlinear_pa_kernel(tc, x, q_prev, v, out):
             )
 
         def w_products(g, strips):
-            for strip in strips:
-                bank = new_bank(("w", g, strip), [P, PACK, P])
-                cols = slice(strip * P, (strip + 1) * P)
+            for first in range(0, len(strips), 2):
+                pair = strips[first : first + 2]
+                for strip in pair:
+                    new_bank(("w", g, strip), [P, PACK, P])
                 for t in range(PACK):
                     places = slice(g * K_PASS + t * P, g * K_PASS + (t + 1) * P)
                     for c in range(PASSES):
-                        nc.tensor.matmul_mx(
-                            out=bank[:, t, :],
-                            lhsT=q_words[:, c, places].bitcast(FP8X4),
-                            lhsT_scale=q_scales[:, c, places],
-                            rhs=h_words[:, c, cols].bitcast(FP8X4),
-                            rhs_scale=h_scales[:, c, cols],
-                            start=(c == 0),
-                            stop=(c == PASSES - 1),
-                        )
+                        for strip in pair:
+                            cols = slice(strip * P, (strip + 1) * P)
+                            nc.tensor.matmul_mx(
+                                out=banks[("w", g, strip)][:, t, :],
+                                lhsT=q_words[:, c, places].bitcast(FP8X4),
+                                lhsT_scale=q_scales[:, c, places],
+                                rhs=h_words[:, c, cols].bitcast(FP8X4),
+                                rhs_scale=h_scales[:, c, cols],
+                                start=(c == 0),
+                                stop=(c == PASSES - 1),
+                            )
 
         def w_copies(g, strips, on_vector):
             for strip in strips:

@@ -61,10 +61,12 @@ def tile_householderlinear_pa_kernel(tc, x, q_prev, v, out):
 
         load_q(0, 0)
         load_q(1, 0)
-        for first in range(0, ROW_TILES, 2):
-            load_x(first)
+        load_x(0)
+        load_x(2)
+        load_x(4)
         load_q(0, 1)
         load_q(1, 1)
+        load_x(6)
 
         dummy_in = const.tile([P, 1], F32)
         dummy_out = const.tile([P, 1], F32)
@@ -289,36 +291,41 @@ def tile_householderlinear_pa_kernel(tc, x, q_prev, v, out):
 
         turn_x((0, 1))
         quantise_h(0)
+        quantise_q(0)
         h_products((6,))
         h_copies((6,))
-        turn_x((2, 3, 4, 5))
+        turn_x((2, 3))
         h_products((7,))
-        quantise_q(0)
+        quantise_h(1)
+        quantise_h(2)
         h_copies((7,))
-        turn_x((6, 7))
-        regroup_q(1, 1, 1, on_vector=False)
+        turn_x((4, 5))
 
-        for strip_pair in range(3):
-            strips = (2 * strip_pair, 2 * strip_pair + 1)
-            w_products(0, strips)
-            w_copies(0, strips, False)
-            quantise_h(strip_pair + 1)
-            regroup_q(strip_pair // 2, 1, strip_pair % 2)
+        regroup_q(1, 1, 1, on_vector=False)
+        w_products(0, range(6))
+        w_copies(0, range(6), False)
+        regroup_q(0, 1, 0)
+        quantise_h(3)
+        regroup_q(0, 1, 1)
+        regroup_q(1, 1, 0)
         quantise_q(1)
         w_products(0, (6, 7))
+        x_transposes((6, 7))
 
         w_copies(0, (6,), True)
         quantise_x(0)
         w_copies(0, (7,), True)
         quantise_w(0, 0)
+        x_copy(6, False)
+        w_products(1, range(4))
+        w_copies(1, (0, 1, 3), False)
+        w_copies(1, (2,), True)
         quantise_x(2)
-        w_products(1, (0, 1, 2, 3))
-        w_copies(1, (0, 1, 2), False)
-        w_copies(1, (3,), True)
         quantise_w(1, 0)
         quantise_w(0, 1)
-        w_products(1, (4, 5, 6, 7))
-        w_copies(1, (4, 5, 6, 7), False)
+        x_copy(7, False)
+        w_products(1, range(4, 8))
+        w_copies(1, range(4, 8), False)
 
         for side in range(SIDES):
             for r in range(ROW_TILES):

@@ -25,7 +25,7 @@ SIDES = N // BANK
 STRIPS = N // P
 ROW_TILES = N // P
 WARM_UPS = 3
-PLAIN_STRIPS = (0, 1)
+PLAIN_STRIPS = (0, 1, 4)
 
 
 def tile_householderlinear_pa_kernel(tc, x, q_prev, v, out):
@@ -142,40 +142,35 @@ def tile_householderlinear_pa_kernel(tc, x, q_prev, v, out):
                 out=minus_half_diag[:], in_=ident[:], func=COPY, scale=minus_half_sum[:, 0:1]
             )
 
-        def passes_of(strip):
-            return (1, 0) if strip < PACK else (0, 1)
-
-        def h_products(strips):
-            for strip in strips:
-                for c in passes_of(strip):
-                    bank = new_bank(("h", c, strip), [P, PACK, P])
-                    for t in range(PACK):
-                        j_strip = PACK * c + t
-                        add_identity = j_strip == strip and strip in PLAIN_STRIPS
+        def h_products(blocks):
+            for c, strip in blocks:
+                bank = new_bank(("h", c, strip), [P, PACK, P])
+                for t in range(PACK):
+                    j_strip = PACK * c + t
+                    add_identity = j_strip == strip and strip in PLAIN_STRIPS
+                    nc.tensor.matmul(
+                        out=bank[:, t, :],
+                        lhsT=v_row[:, j_strip * P : (j_strip + 1) * P],
+                        rhs=v_row[:, strip * P : (strip + 1) * P],
+                        start=True,
+                        stop=not add_identity,
+                    )
+                    if add_identity:
                         nc.tensor.matmul(
-                            out=bank[:, t, :],
-                            lhsT=v_row[:, j_strip * P : (j_strip + 1) * P],
-                            rhs=v_row[:, strip * P : (strip + 1) * P],
-                            start=True,
-                            stop=not add_identity,
+                            out=bank[:, t, :], lhsT=ident[:], rhs=minus_half_diag[:], start=False, stop=True
                         )
-                        if add_identity:
-                            nc.tensor.matmul(
-                                out=bank[:, t, :], lhsT=ident[:], rhs=minus_half_diag[:], start=False, stop=True
-                            )
 
-        def h_copies(strips):
-            for strip in strips:
-                for c in passes_of(strip):
-                    dst = h_bf[:, c, strip * P : (strip + 1) * P, :]
-                    src = banks[("h", c, strip)][:].rearrange("p t i -> p i t")
-                    d = strip - PACK * c
-                    if 0 <= d < PACK and strip not in PLAIN_STRIPS:
-                        nc.vector.scalar_tensor_tensor(
-                            out=dst, in0=src, scalar=coeff[:, 0:1], in1=diag_view(d), op0=MULT, op1=ADD
-                        )
-                    else:
-                        nc.scalar.activation(out=dst, in_=src, func=COPY, scale=coeff[:, 0:1])
+        def h_copies(blocks):
+            for c, strip in blocks:
+                dst = h_bf[:, c, strip * P : (strip + 1) * P, :]
+                src = banks[("h", c, strip)][:].rearrange("p t i -> p i t")
+                d = strip - PACK * c
+                if 0 <= d < PACK and strip not in PLAIN_STRIPS:
+                    nc.vector.scalar_tensor_tensor(
+                        out=dst, in0=src, scalar=coeff[:, 0:1], in1=diag_view(d), op0=MULT, op1=ADD
+                    )
+                else:
+                    nc.scalar.activation(out=dst, in_=src, func=COPY, scale=coeff[:, 0:1])
 
         def quantise_h(strip_pair):
             cols = slice(2 * strip_pair * P, (2 * strip_pair + 2) * P)
@@ -255,9 +250,9 @@ def tile_householderlinear_pa_kernel(tc, x, q_prev, v, out):
                 w_bf[:, g, cols, :].rearrange("p i t -> p (i t)"), w_words[:, g, cols], w_scales[:, g, cols]
             )
 
-        def out_bank(r, side):
-            bank = new_bank(("o", r, side), [P, BANK])
-            cols = slice(side * BANK, (side + 1) * BANK)
+        def out_bank(r, first, width, on_vector):
+            bank = new_bank(("o", r, first), [P, width])
+            cols = slice(first, first + width)
             for g in range(PASSES):
                 nc.tensor.matmul_mx(
                     out=bank[:],
@@ -268,21 +263,21 @@ def tile_householderlinear_pa_kernel(tc, x, q_prev, v, out):
                     start=(g == 0),
                     stop=(g == PASSES - 1),
                 )
-            copy_on(r % 2 == 0, out_sb[:, r, cols], bank[:])
+            copy_on(on_vector, out_sb[:, r, cols], bank[:])
             nc.sync.dma_start(out=out_view[:, r, cols], in_=out_sb[:, r, cols])
 
         warm_up()
         sum_of_squares()
         nc.vector.tensor_copy(out=v_row[0:1, :], in_=v_one[:])
         reflection_coeff()
-        h_products((0, 1))
-        h_copies((0, 1))
-        for c in range(PASSES):
-            for u in range(2):
-                regroup_q(c, 0, u)
-        for strips in ((2, 3), (4, 5)):
-            h_products(strips)
-            h_copies(strips)
+        h_products(((1, 0), (1, 1), (0, 0), (0, 2), (0, 1), (0, 3), (1, 2), (1, 3)))
+        h_copies(((1, 0), (1, 1), (0, 0), (0, 1), (1, 2), (1, 3)))
+        for c, strip in ((0, 2), (1, 3)):
+            regroup_q(c, 0, 0)
+            regroup_q(c, 0, 1)
+            h_copies(((0, strip),))
+        h_products(((0, 4), (1, 4), (0, 5), (1, 5)))
+        h_copies(((0, 4), (0, 5), (1, 4), (1, 5)))
 
         def turn_x(row_tiles):
             x_transposes(row_tiles)
@@ -292,13 +287,13 @@ def tile_householderlinear_pa_kernel(tc, x, q_prev, v, out):
         turn_x((0, 1))
         quantise_h(0)
         quantise_q(0)
-        h_products((6,))
-        h_copies((6,))
+        h_products(((0, 6), (1, 6)))
+        h_copies(((0, 6), (1, 6)))
         turn_x((2, 3))
-        h_products((7,))
+        h_products(((0, 7), (1, 7)))
         quantise_h(1)
         quantise_h(2)
-        h_copies((7,))
+        h_copies(((0, 7), (1, 7)))
         turn_x((4, 5))
 
         regroup_q(1, 1, 1, on_vector=False)
@@ -324,15 +319,24 @@ def tile_householderlinear_pa_kernel(tc, x, q_prev, v, out):
         quantise_w(1, 0)
         quantise_w(0, 1)
         x_copy(7, False)
-        w_products(1, range(4, 8))
-        w_copies(1, range(4, 8), False)
+        w_products(1, (4, 5))
+        w_copies(1, (4, 5), False)
+        w_products(1, (6,))
+        w_copies(1, (6,), False)
 
         for side in range(SIDES):
             for r in range(ROW_TILES):
-                out_bank(r, side)
+                if (r, side) == (ROW_TILES - 1, SIDES - 1):
+                    out_bank(r, side * BANK, BANK // 2, False)
+                    out_bank(r, side * BANK + BANK // 2, BANK // 2, True)
+                else:
+                    out_bank(r, side * BANK, BANK, r % 2 == 0)
                 if (r, side) == (0, 0):
                     quantise_x(4)
                 if (r, side) == (2, 0):
                     quantise_x(6)
+                if (r, side) == (3, 0):
+                    w_products(1, (7,))
+                    w_copies(1, (7,), False)
                 if (r, side) == (4, 0):
                     quantise_w(1, 1)

@@ -270,14 +270,14 @@ def tile_householderlinear_pa_kernel(tc, x, q_prev, v, out):
         sum_of_squares()
         nc.vector.tensor_copy(out=v_row[0:1, :], in_=v_one[:])
         reflection_coeff()
-        h_products(((1, 0), (1, 1), (0, 0), (0, 2), (0, 1), (0, 3), (1, 2), (1, 3)))
-        h_copies(((1, 0), (1, 1), (0, 0), (0, 1), (1, 2), (1, 3)))
+        h_products(((1, 0), (1, 1), (0, 2), (1, 2), (1, 3), (0, 3), (0, 0), (0, 1)))
+        h_copies(((1, 0), (1, 1), (1, 2), (1, 3), (0, 0), (0, 1)))
         for c, strip in ((0, 2), (1, 3)):
             regroup_q(c, 0, 0)
             regroup_q(c, 0, 1)
             h_copies(((0, strip),))
-        h_products(((0, 4), (1, 4), (0, 5), (1, 5)))
-        h_copies(((0, 4), (0, 5), (1, 4), (1, 5)))
+        h_products(((0, 4), (1, 5), (0, 5), (1, 4)))
+        h_copies(((0, 4), (1, 5), (0, 5), (1, 4)))
 
         def turn_x(row_tiles):
             x_transposes(row_tiles)
@@ -298,7 +298,7 @@ def tile_householderlinear_pa_kernel(tc, x, q_prev, v, out):
 
         regroup_q(1, 1, 1, on_vector=False)
         w_products(0, range(6))
-        w_copies(0, range(6), False)
+        w_copies(0, range(5), False)
         regroup_q(0, 1, 0)
         quantise_h(3)
         regroup_q(0, 1, 1)
@@ -307,7 +307,7 @@ def tile_householderlinear_pa_kernel(tc, x, q_prev, v, out):
         w_products(0, (6, 7))
         x_transposes((6, 7))
 
-        w_copies(0, (6,), True)
+        w_copies(0, (5, 6), True)
         quantise_x(0)
         w_copies(0, (7,), True)
         quantise_w(0, 0)

@@ -314,8 +314,8 @@ def tile_householderlinear_pa_kernel(tc, x, q_prev, v, out):
         x_copy(6, False)
         w_products(1, range(4))
         w_copies(1, (0, 1, 3), False)
-        w_copies(1, (2,), True)
         quantise_x(2)
+        w_copies(1, (2,), True)
         quantise_w(1, 0)
         quantise_w(0, 1)
         x_copy(7, False)

from contextlib import ExitStack

import concourse.mybir as mybir
from concourse.masks import make_identity

FLOPS = 2 * 2 * 1024 * 1024 * 1024

F32 = mybir.dt.float32
BF16 = mybir.dt.bfloat16
U32 = mybir.dt.uint32
U8 = mybir.dt.uint8
I32 = mybir.dt.int32
FP8X4 = mybir.dt.float8_e4m3fn_x4
MULT = mybir.AluOpType.mult
ADD = mybir.AluOpType.add
COPY = mybir.ActivationFunctionType.Copy

P = 128
N = 1024
PACK = 4
K_PASS = P * PACK
PASSES = N // K_PASS
BANK = 512
SIDES = N // BANK
STRIPS = N // P
ROW_TILES = N // P
WARM_UPS = 3
PLAIN_STRIPS = (0, 1, 4)


def tile_householderlinear_pa_kernel(tc, x, q_prev, v, out):
    nc = tc.nc
    with ExitStack() as ctx:
        ctx.enter_context(tc.manual_schedule())
        const = ctx.enter_context(tc.tile_pool(name="const", bufs=1))
        keep = ctx.enter_context(tc.tile_pool(name="keep", bufs=1))
        psum = ctx.enter_context(tc.psum_pool(name="psum", bufs=8))

        v_cols = const.tile([P, N // P], BF16)
        nc.sync.dma_start(out=v_cols[:], in_=v.rearrange("(p m) -> p m", p=P))
        v_one = const.tile([1, N], BF16)
        nc.sync.dma_start(out=v_one[:], in_=v.rearrange("(o n) -> o n", o=1))
        v_row = const.tile([P, N], BF16)
        nc.vector.memset(v_row[:].bitcast(I32), 0)

        q_view = q_prev.rearrange("(c t p) k -> c p t k", c=PASSES, t=PACK, p=P)
        q_raw = {}
        for c in range(PASSES):
            for g in range(SIDES):
                q_raw[(c, g)] = keep.tile([P, PACK, BANK], BF16, name="q_raw%d%d" % (c, g))
        x_view = x.rearrange("(p r) k -> p r k", r=ROW_TILES)
        out_view = out.rearrange("(p r) i -> p r i", r=ROW_TILES)
        x_raw = keep.tile([P, ROW_TILES, N], BF16)

        def load_q(c, g):
            nc.sync.dma_start(out=q_raw[(c, g)][:], in_=q_view[c][:, :, g * BANK : (g + 1) * BANK])

        def load_x(first):
            rows = slice(first, first + 2)
            nc.sync.dma_start(out=x_raw[:, rows, :], in_=x_view[:, rows, :])

        load_q(0, 0)
        load_q(1, 0)
        load_x(0)
        load_x(2)
        load_x(4)
        load_q(0, 1)
        load_q(1, 1)
        load_x(6)

        dummy_in = const.tile([P, 1], F32)
        dummy_out = const.tile([P, 1], F32)
        zeros = const.tile([P, BANK], BF16)
        nc.gpsimd.memset(zeros[:].bitcast(I32), 0)
        nc.gpsimd.memset(dummy_in[:], 0.0)
        nc.scalar.activation(out=dummy_out[:], in_=dummy_in[:], func=COPY)
        ident = const.tile([P, P], F32)
        make_identity(nc, ident[:])
        diag = const.tile([P, (P + 1) * PACK], BF16)
        nc.vector.memset(diag[:].bitcast(I32), 0)

        def diag_view(d):
            first = PACK - 1 - d
            return diag[:, first : first + P * PACK].rearrange("p (i t) -> p i t", t=PACK)

        nc.vector.tensor_copy(out=diag_view(0)[:, :, 0], in_=ident[:])
        minus_half_sum = const.tile([P, 1], F32)
        minus_half_diag = const.tile([P, P], F32)
        coeff = const.tile([P, 1], F32)

        h_bf = keep.tile([P, PASSES, N, PACK], BF16, align_bytes=64)
        h_words = keep.tile([P, PASSES, N], U32, align_bytes=64)
        h_scales = keep.tile([P, PASSES, N], U8, align_bytes=64)
        q_bf = keep.tile([P, PASSES, N, PACK], BF16, align_bytes=64)
        q_words = keep.tile([P, PASSES, N], U32, align_bytes=64)
        q_scales = keep.tile([P, PASSES, N], U8, align_bytes=64)
        x_bf = keep.tile([P, ROW_TILES, N], BF16, align_bytes=64)
        x_words = keep.tile([P, ROW_TILES, PASSES, P], U32, align_bytes=64)
        x_scales = keep.tile([P, ROW_TILES, PASSES, P], U8, align_bytes=64)
        w_bf = keep.tile([P, PASSES, N, PACK], BF16, align_bytes=64)
        w_words = keep.tile([P, PASSES, N], U32, align_bytes=64)
        w_scales = keep.tile([P, PASSES, N], U8, align_bytes=64)
        out_sb = keep.tile([P, ROW_TILES, N], F32)

        banks = {}

        def new_bank(key, shape):
            banks[key] = psum.tile(shape, F32, tag="bank", name="bank_%s%d" % (key[0], len(banks)))
            return banks[key]

        def copy_on(on_vector, dst, src):
            if on_vector:
                nc.vector.tensor_copy(out=dst, in_=src)
            else:
                nc.scalar.copy(out=dst, in_=src)

        def quantise(src, words, scales):
            nc.vector.quantize_mx(out=words.bitcast(FP8X4), scales=scales, in_=src)

        def warm_up():
            bank = new_bank(("z",), [P, BANK])
            for m in range(WARM_UPS):
                nc.tensor.matmul(out=bank[:], lhsT=zeros[:, :P], rhs=zeros[:], start=True, stop=True)

        def sum_of_squares():
            total = new_bank(("s",), [P, 1])
            for m in range(N // P):
                nc.tensor.matmul(
                    out=total[:],
                    lhsT=v_cols[:, m : m + 1].to_broadcast([P, P]),
                    rhs=v_cols[:, m : m + 1],
                    start=(m == 0),
                    stop=(m == N // P - 1),
                )

        def reflection_coeff():
            nc.vector.tensor_scalar(
                out=minus_half_sum[:], in0=banks[("s",)][:], scalar1=-0.5, scalar2=None, op0=MULT
            )
            nc.vector.reciprocal(out=coeff[:], in_=minus_half_sum[:])
            nc.scalar.activation(
                out=minus_half_diag[:], in_=ident[:], func=COPY, scale=minus_half_sum[:, 0:1]
            )

        def h_products(blocks):
            for c, strip in blocks:
                bank = new_bank(("h", c, strip), [P, PACK, P])
                for t in range(PACK):
                    j_strip = PACK * c + t
                    add_identity = j_strip == strip and strip in PLAIN_STRIPS
                    nc.tensor.matmul(
                        out=bank[:, t, :],
                        lhsT=v_row[:, j_strip * P : (j_strip + 1) * P],
                        rhs=v_row[:, strip * P : (strip + 1) * P],
                        start=True,
                        stop=not add_identity,
                    )
                    if add_identity:
                        nc.tensor.matmul(
                            out=bank[:, t, :], lhsT=ident[:], rhs=minus_half_diag[:], start=False, stop=True
                        )

        def h_copies(blocks):
            for c, strip in blocks:
                dst = h_bf[:, c, strip * P : (strip + 1) * P, :]
                src = banks[("h", c, strip)][:].rearrange("p t i -> p i t")
                d = strip - PACK * c
                if 0 <= d < PACK and strip not in PLAIN_STRIPS:
                    nc.vector.scalar_tensor_tensor(
                        out=dst, in0=src, scalar=coeff[:, 0:1], in1=diag_view(d), op0=MULT, op1=ADD
                    )
                else:
                    nc.scalar.activation(out=dst, in_=src, func=COPY, scale=coeff[:, 0:1])

        def quantise_h(strip_pair):
            cols = slice(2 * strip_pair * P, (2 * strip_pair + 2) * P)
            for c in range(PASSES):
                quantise(
                    h_bf[:, c, cols, :].rearrange("p i t -> p (i t)"), h_words[:, c, cols], h_scales[:, c, cols]
                )

        def regroup_q(c, g, u, on_vector=True):
            cols = slice(2 * u * P, (2 * u + 2) * P)
            places = slice(g * K_PASS + 2 * u * P, g * K_PASS + (2 * u + 2) * P)
            copy_on(
                on_vector,
                q_bf[:, c, places, :].rearrange("p (e n i) t -> p e n t i", e=2, i=4),
                q_raw[(c, g)][:, :, cols].rearrange("p t (n i e) -> p e n t i", e=2, i=4),
            )

        def quantise_q(g):
            places = slice(g * K_PASS, (g + 1) * K_PASS)
            for c in range(PASSES):
                quantise(
                    q_bf[:, c, places, :].rearrange("p k t -> p (k t)"),
                    q_words[:, c, places],
                    q_scales[:, c, places],
                )

        def x_transposes(row_tiles):
            for r in row_tiles:
                bank = new_bank(("x", r), [P, PACK, P])
                words = x_raw[:, r, :].bitcast(F32)
                for gu in range(PACK):
                    nc.tensor.transpose(bank[:, gu, :], words[:, gu * P : (gu + 1) * P], ident[:])

        def x_copy(r, on_vector):
            copy_on(
                on_vector,
                x_bf[:, r, :].bitcast(F32).rearrange("p (g b u) -> p g b u", g=PASSES, u=2),
                banks[("x", r)][:].rearrange("p (g u) b -> p g b u", g=PASSES),
            )

        def quantise_x(first):
            rows = slice(first, first + 2)
            quantise(
                x_bf[:, rows, :].rearrange("p r k -> p (r k)"),
                x_words[:, rows].rearrange("p r g b -> p (r g b)"),
                x_scales[:, rows].rearrange("p r g b -> p (r g b)"),
            )

        def w_products(g, strips):
            for first in range(0, len(strips), 2):
                pair = strips[first : first + 2]
                for strip in pair:
                    new_bank(("w", g, strip), [P, PACK, P])
                for t in range(PACK):
                    places = slice(g * K_PASS + t * P, g * K_PASS + (t + 1) * P)
                    for c in range(PASSES):
                        for strip in pair:
                            cols = slice(strip * P, (strip + 1) * P)
                            nc.tensor.matmul_mx(
                                out=banks[("w", g, strip)][:, t, :],
                                lhsT=q_words[:, c, places].bitcast(FP8X4),
                                lhsT_scale=q_scales[:, c, places],
                                rhs=h_words[:, c, cols].bitcast(FP8X4),
                                rhs_scale=h_scales[:, c, cols],
                                start=(c == 0),
                                stop=(c == PASSES - 1),
                            )

        def w_copies(g, strips, on_vector):
            for strip in strips:
                cols = slice(strip * P, (strip + 1) * P)
                copy_on(on_vector, w_bf[:, g, cols, :], banks[("w", g, strip)][:].rearrange("p t i -> p i t"))

        def quantise_w(g, side):
            cols = slice(side * BANK, (side + 1) * BANK)
            quantise(
                w_bf[:, g, cols, :].rearrange("p i t -> p (i t)"), w_words[:, g, cols], w_scales[:, g, cols]
            )

        def out_bank(r, first, width, on_vector):
            bank = new_bank(("o", r, first), [P, width])
            cols = slice(first, first + width)
            for g in range(PASSES):
                nc.tensor.matmul_mx(
                    out=bank[:],
                    lhsT=x_words[:, r, g, :].bitcast(FP8X4),
                    lhsT_scale=x_scales[:, r, g, :],
                    rhs=w_words[:, g, cols].bitcast(FP8X4),
                    rhs_scale=w_scales[:, g, cols],
                    start=(g == 0),
                    stop=(g == PASSES - 1),
                )
            copy_on(on_vector, out_sb[:, r, cols], bank[:])
            nc.sync.dma_start(out=out_view[:, r, cols], in_=out_sb[:, r, cols])

        warm_up()
        sum_of_squares()
        nc.vector.tensor_copy(out=v_row[0:1, :], in_=v_one[:])
        reflection_coeff()
        h_products(((1, 0), (1, 1), (0, 2), (1, 2), (1, 3), (0, 3), (0, 0), (0, 1)))
        h_copies(((1, 0), (1, 1), (1, 2), (1, 3), (0, 0), (0, 1)))
        for c, strip in ((0, 2), (1, 3)):
            regroup_q(c, 0, 0)
            regroup_q(c, 0, 1)
            h_copies(((0, strip),))
        h_products(((0, 4), (1, 5), (0, 5), (1, 4)))
        h_copies(((0, 4), (1, 5), (0, 5), (1, 4)))

        def turn_x(row_tiles):
            x_transposes(row_tiles)
            for r in row_tiles:
                x_copy(r, False)

        turn_x((0, 1))
        quantise_h(0)
        quantise_q(0)
        h_products(((0, 6), (1, 6)))
        h_copies(((0, 6), (1, 6)))
        turn_x((2, 3))
        h_products(((0, 7), (1, 7)))
        quantise_h(1)
        quantise_h(2)
        h_copies(((0, 7), (1, 7)))
        turn_x((4, 5))

        regroup_q(1, 1, 1, on_vector=False)
        w_products(0, range(6))
        w_copies(0, range(5), False)
        regroup_q(0, 1, 0)
        quantise_h(3)
        regroup_q(0, 1, 1)
        regroup_q(1, 1, 0)
        quantise_q(1)
        w_products(0, (6, 7))
        x_transposes((6, 7))

        w_copies(0, (5, 6), True)
        quantise_x(0)
        w_copies(0, (7,), True)
        quantise_w(0, 0)
        x_copy(6, False)
        w_products(1, range(4))
        w_copies(1, (0, 1, 3), False)
        quantise_x(2)
        w_copies(1, (2,), True)
        quantise_w(1, 0)
        quantise_w(0, 1)
        x_copy(7, False)
        w_products(1, (4, 5))
        w_copies(1, (4, 5), False)
        w_products(1, (6,))
        w_copies(1, (6,), False)

        for side in range(SIDES):
            for r in range(ROW_TILES):
                if (r, side) == (ROW_TILES - 1, SIDES - 1):
                    out_bank(r, side * BANK, BANK // 2, False)
                    out_bank(r, side * BANK + BANK // 2, BANK // 2, True)
                else:
                    out_bank(r, side * BANK, BANK, r % 2 == 0)
                if (r, side) == (0, 0):
                    quantise_x(4)
                if (r, side) == (2, 0):
                    quantise_x(6)
                if (r, side) == (3, 0):
                    w_products(1, (7,))
                    w_copies(1, (7,), False)
                if (r, side) == (4, 0):
                    quantise_w(1, 1)
